import numpy as np
import ml_dtypes


def mxq(x, axis, fmt="e4m3"):
    dtype, down = {"e4m3": (ml_dtypes.float8_e4m3fn, 7), "e5m2": (ml_dtypes.float8_e5m2, 14)}[fmt]
    v = np.moveaxis(np.asarray(x, np.float32).astype(ml_dtypes.bfloat16).astype(np.float64), axis, -1)
    blocks = v.reshape(v.shape[:-1] + (-1, 32))
    amax = np.abs(blocks).max(-1, keepdims=True)
    byte = np.maximum(np.where(amax > 0, np.frexp(amax)[1] - 1 + 127, 0) - down, 1)
    scale = np.exp2(byte - 127.0)
    codes = (blocks / scale).astype(np.float32).astype(dtype).astype(np.float64)
    return np.moveaxis((codes * scale).reshape(v.shape), -1, axis)


WIDE = False


def mx_kscale(k):
    if not WIDE:
        return np.ones(k)
    levels = np.array([10, -10, 5, -5, 0])
    a = np.random.permutation(np.resize(levels, k // 512 * 4)).reshape(k // 512, 4)
    idx = np.arange(k)
    return np.exp2(a[idx // 512, idx % 128 // 32])


BF16 = ml_dtypes.bfloat16


def bf(x):
    return np.asarray(x, np.float32).astype(BF16)


def f64(x):
    return np.asarray(x).astype(np.float64)


B, C, E, H, HS, WS = 4, 128, 512, 16, 64, 64
N = HS * WS
EPS = 1e-5
A = 2.0 * (E / H) ** -0.5 / np.sqrt(N)


def chan_layernorm(x, g):
    mean = x.mean(axis=1, keepdims=True)
    var = x.var(axis=1, keepdims=True)
    return (x - mean) * (1.0 / np.sqrt(var + EPS)) * g


def setup_inputs():
    s = mx_kscale(E)
    return {"h_attn": bf(np.random.standard_normal((B, E, HS, WS)) * A * s[None, :, None, None]),
            "xn": bf(np.random.standard_normal((B, C, HS, WS))),
            "Wout": bf(np.random.standard_normal((C, E)) / (np.sqrt(E) * A) / s[None, :]),
            "bout": bf(0.3 * np.random.standard_normal(C)),
            "outnorm_g": bf(1.0 + 0.1 * np.random.standard_normal((1, C, 1, 1)))}


def reference(h_attn, xn, Wout, bout, outnorm_g):
    a = f64(h_attn).reshape(B, E, N)
    y = (mxq(f64(Wout), 1, "e4m3") @ mxq(a, 1, "e4m3")) + f64(bout)[None, :, None]
    y = y.reshape(B, C, HS, WS)
    return chan_layernorm(y, f64(outnorm_g)) + f64(xn)

@@ -1,0 +1,196 @@
+from contextlib import ExitStack
+
+import concourse.mybir as mybir
+from concourse.masks import make_identity
+
+F32 = mybir.dt.float32
+BF16 = mybir.dt.bfloat16
+U32 = mybir.dt.uint32
+U8 = mybir.dt.uint8
+FP8X4 = mybir.dt.float8_e4m3fn_x4
+ALU = mybir.AluOpType
+ACT = mybir.ActivationFunctionType
+AX = mybir.AxisListType
+
+P = 128
+B, C, E, N = 4, 128, 512, 4096
+PACK = 4
+CH = 512
+NBLK = CH // P
+EPS = 1e-5
+FLOPS = 2 * C * E * B * N
+
+S_REGROUP = (1, 3, 5, 7, 9, 11, 13, 15, 17, 19, 21, 23, 25, 27, 29, 31)
+
+
+def tile_linearattention_pb_t_kernel(tc, h_attn, xn, Wout, bout, outnorm_g, out):
+    nc = tc.nc
+    with ExitStack() as ctx:
+        const = ctx.enter_context(tc.tile_pool(name="const", bufs=1))
+        rawp = ctx.enter_context(tc.tile_pool(name="rawp", bufs=4))
+        xnp = ctx.enter_context(tc.tile_pool(name="xnp", bufs=2))
+        grp = ctx.enter_context(tc.tile_pool(name="grp", bufs=4))
+        cdp = ctx.enter_context(tc.tile_pool(name="cdp", bufs=3))
+        tp = ctx.enter_context(tc.tile_pool(name="tp", bufs=4))
+        zp = ctx.enter_context(tc.tile_pool(name="zp", bufs=4))
+        op = ctx.enter_context(tc.tile_pool(name="op", bufs=3))
+        smp = ctx.enter_context(tc.tile_pool(name="smp", bufs=3))
+        ps_y = ctx.enter_context(tc.psum_pool(name="ps_y", bufs=2))
+        ps_t = ctx.enter_context(tc.psum_pool(name="ps_t", bufs=4))
+        ps_z = ctx.enter_context(tc.psum_pool(name="ps_z", bufs=2))
+
+        w_sb = const.tile([P, E], BF16)
+        nc.scalar.dma_start(out=w_sb[:], in_=Wout)
+        bg = const.tile([P, P], BF16)
+        nc.vector.memset(bg[:], 0.0)
+        nc.scalar.dma_start(out=bg[0:1, :], in_=bout.unsqueeze(0))
+        nc.scalar.dma_start(out=bg[1:2, :], in_=outnorm_g.rearrange("a c h w -> (a h w) c"))
+
+        loads = []
+        for b in range(B):
+            widths = (512, 512, 1024, 2048) if b == 0 else (2048, 2048)
+            n0 = 0
+            for wl in widths:
+                loads.append((b, n0, wl))
+                n0 += wl
+        raw_of = {}
+        xn_of = {}
+
+        def issue_load(li):
+            b, n0, wl = loads[li]
+            raw = rawp.tile([P, PACK, wl], BF16, name="raw", tag="raw")
+            src = h_attn[b].rearrange("(p j) h w -> p j (h w)", j=PACK)
+            nc.sync.dma_start(out=raw[:], in_=src[:, :, n0:n0 + wl])
+            for k in range(wl // CH):
+                raw_of[(b * N + n0) // CH + k] = (raw, k * CH)
+
+        def issue_xn(b):
+            xt = xnp.tile([P, N], BF16, name="xt", tag="xt")
+            nc.sync.dma_start(out=xt[:], in_=xn[b].rearrange("c h w -> c (h w)"))
+            xn_of[b] = xt
+
+        eps_col = const.tile([P, 1], F32)
+        nc.vector.memset(eps_col[:], EPS)
+        junk = const.tile([P, 1], F32)
+        nc.scalar.activation(out=junk[:], in_=eps_col[:], func=ACT.Sqrt)
+        ident_b = const.tile([P, P], BF16)
+        make_identity(nc, ident_b[:])
+        ident_f = const.tile([P, P], F32)
+        make_identity(nc, ident_f[:])
+
+        issue_load(0)
+        issue_load(1)
+        issue_load(2)
+        issue_xn(0)
+        issue_load(3)
+        next_load = 4
+
+        w_r = const.tile([P, PACK, P], BF16)
+        nc.vector.tensor_copy(out=w_r[:], in_=w_sb[:].rearrange("c (p t) -> c t p", t=PACK))
+        w_ps = ps_z.tile([P, PACK, P], BF16, name="w_ps", tag="zT")
+        for t in range(PACK):
+            nc.tensor.transpose(w_ps[:, t, :], w_r[:, t, :], ident_b[:])
+        w_g = const.tile([P, P, PACK], BF16, align_bytes=64)
+        nc.vector.tensor_copy(out=w_g[:], in_=w_ps[:].rearrange("p t c -> p c t"))
+        w_codes = const.tile([P, P], U32, align_bytes=64)
+        w_scales = const.tile([P, P], U8, align_bytes=64)
+        nc.vector.quantize_mx(out=w_codes[:].bitcast(FP8X4), scales=w_scales[:],
+                              in_=w_g[:].rearrange("p c t -> p (c t)"))
+        bg_ps = ps_z.tile([P, P], BF16, name="bg_ps", tag="zT")
+        nc.tensor.transpose(bg_ps[:], bg[:], ident_b[:])
+        bgf = const.tile([P, 2], F32)
+        nc.vector.tensor_copy(out=bgf[:], in_=bg_ps[:, 0:2])
+        b_col = bgf[:, 0:1]
+        g_col = bgf[:, 1:2]
+
+        stores = []
+        for b in range(B):
+            widths = (2048, 1024, 512, 512) if b == B - 1 else (2048, 2048)
+            n0 = 0
+            for wl in widths:
+                stores.append((b, n0, wl))
+                n0 += wl
+        store_of = {}
+        for si, (b, n0, wl) in enumerate(stores):
+            for k in range(wl // CH):
+                store_of[(b * N + n0) // CH + k] = (si, k * CH, k == wl // CH - 1)
+        o_tiles = {}
+
+        n_chunks = B * N // CH
+        for pair in range(n_chunks // 2):
+            chunks = (2 * pair, 2 * pair + 1)
+            st = smp.tile([P, 2 * NBLK, 6], F32, name="st", tag="st")
+            tTs = []
+            for ci, c in enumerate(chunks):
+                if c not in raw_of:
+                    issue_load(next_load)
+                    next_load += 1
+                b = c * CH // N
+                if b not in xn_of:
+                    issue_xn(b)
+                raw, off = raw_of[c]
+                g = grp.tile([P, CH, PACK], BF16, name="g", tag="g", align_bytes=64)
+                dst = g[:].rearrange("p (c i) t -> p c t i", i=4)
+                src = raw[:, :, off:off + CH].rearrange("p t (c i) -> p c t i", i=4)
+                if c in S_REGROUP:
+                    nc.scalar.copy(out=dst, in_=src)
+                else:
+                    nc.vector.tensor_copy(out=dst, in_=src)
+                codes = cdp.tile([P, CH], U32, name="codes", tag="codes", align_bytes=64)
+                scales = cdp.tile([P, CH], U8, name="scales", tag="scales", align_bytes=64)
+                nc.vector.quantize_mx(out=codes[:].bitcast(FP8X4), scales=scales[:],
+                                      in_=g[:].rearrange("p w t -> p (w t)"))
+                y = ps_y.tile([P, CH], F32, name="y", tag="y")
+                nc.tensor.matmul_mx(out=y[:], lhsT=w_codes[:].bitcast(FP8X4), lhsT_scale=w_scales[:],
+                                    rhs=codes[:].bitcast(FP8X4), rhs_scale=scales[:],
+                                    start=True, stop=True)
+                t = tp.tile([P, CH], F32, name="t", tag="t")
+                nc.scalar.activation(out=t[:], in_=y[:], func=ACT.Identity, bias=b_col, scale=1.0)
+                tT = ps_t.tile([P, NBLK, P], F32, name="tT", tag="tT")
+                for k in range(NBLK):
+                    nc.tensor.transpose(tT[:, k, :], t[:, k * P:(k + 1) * P], ident_f[:])
+                for k in range(NBLK):
+                    nc.vector.bn_stats(out=st[:, ci * NBLK + k, :], in_=tT[:, k, :])
+                tTs.append(tT)
+
+            nb = 2 * NBLK
+            sm = smp.tile([P, nb, 3], F32, name="sm", tag="sm")
+            nc.vector.tensor_reduce(out=sm[:], in_=st[:].rearrange("p b (h s) -> p b s h", h=2),
+                                    axis=AX.X, op=ALU.add)
+            d = smp.tile([P, nb], F32, name="d", tag="d")
+            nc.vector.tensor_tensor(out=d[:], in0=st[:, :, 1], in1=st[:, :, 4], op=ALU.subtract)
+            dd = smp.tile([P, nb], F32, name="dd", tag="dd")
+            nc.vector.tensor_tensor(out=dd[:], in0=d[:], in1=d[:], op=ALU.mult)
+            v = smp.tile([P, nb], F32, name="v", tag="v")
+            nc.vector.scalar_tensor_tensor(out=v[:], in0=dd[:], scalar=float(C) / 4.0, in1=sm[:, :, 2],
+                                           op0=ALU.mult, op1=ALU.add)
+            sd = smp.tile([P, nb], F32, name="sd", tag="sd")
+            nc.scalar.activation(out=sd[:], in_=v[:], func=ACT.Sqrt, bias=eps_col[:], scale=1.0 / C)
+            rstd = smp.tile([P, nb], F32, name="rstd", tag="rstd")
+            nc.vector.reciprocal(out=rstd[:], in_=sd[:])
+            nmr = smp.tile([P, nb], F32, name="nmr", tag="nmr")
+            nc.vector.scalar_tensor_tensor(out=nmr[:], in0=sm[:, :, 1], scalar=-0.5, in1=rstd[:],
+                                           op0=ALU.mult, op1=ALU.mult)
+
+            for ci, c in enumerate(chunks):
+                b = c * CH // N
+                tT = tTs[ci]
+                z = zp.tile([P, NBLK, P], F32, name="z", tag="z")
+                for k in range(NBLK):
+                    j = ci * NBLK + k
+                    nc.scalar.activation(out=z[:, k, :], in_=tT[:, k, :], func=ACT.Identity,
+                                         bias=nmr[:, j:j + 1], scale=rstd[:, j:j + 1])
+                zT = ps_z.tile([P, CH], F32, name="zT", tag="zT")
+                for k in range(NBLK):
+                    nc.tensor.transpose(zT[:, k * P:(k + 1) * P], z[:, k, :], ident_f[:])
+                si, ooff, last = store_of[c]
+                sb, sn0, swl = stores[si]
+                if si not in o_tiles:
+                    o_tiles[si] = op.tile([P, swl], F32, name="o", tag="o")
+                o = o_tiles[si]
+                n_in_img = c * CH - b * N
+                nc.vector.scalar_tensor_tensor(out=o[:, ooff:ooff + CH], in0=zT[:], scalar=g_col,
+                                               in1=xn_of[b][:, n_in_img:n_in_img + CH],
+                                               op0=ALU.mult, op1=ALU.add)
+                if last:
+                    nc.sync.dma_start(out=out[sb].rearrange("c h w -> c (h w)")[:, sn0:sn0 + swl], in_=o[:])

@@ -19,24 +19,31 @@ CH = 512
 NBLK = CH // P
 EPS = 1e-5
 FLOPS = 2 * C * E * B * N
-
-S_REGROUP = (1, 3, 5, 7, 9, 11, 13, 15, 17, 19, 21, 23, 25, 27, 29, 31)
+NCH = B * N // CH
+NPAIR = NCH // 2
+LR = 4
+HEAD = (("V", "V"),)
+STEADY = ("V", "S")
+NV_CHUNKS = ()
 
 
 def tile_linearattention_pb_t_kernel(tc, h_attn, xn, Wout, bout, outnorm_g, out):
     nc = tc.nc
     with ExitStack() as ctx:
+
         const = ctx.enter_context(tc.tile_pool(name="const", bufs=1))
+        rawsp = ctx.enter_context(tc.tile_pool(name="rawsp", bufs=4))
         rawp = ctx.enter_context(tc.tile_pool(name="rawp", bufs=4))
-        xnp = ctx.enter_context(tc.tile_pool(name="xnp", bufs=2))
-        grp = ctx.enter_context(tc.tile_pool(name="grp", bufs=4))
-        cdp = ctx.enter_context(tc.tile_pool(name="cdp", bufs=3))
+        xnp = ctx.enter_context(tc.tile_pool(name="xnp", bufs=3))
+        grp = ctx.enter_context(tc.tile_pool(name="grp", bufs=2))
+        cdp = ctx.enter_context(tc.tile_pool(name="cdp", bufs=6))
         tp = ctx.enter_context(tc.tile_pool(name="tp", bufs=4))
         zp = ctx.enter_context(tc.tile_pool(name="zp", bufs=4))
         op = ctx.enter_context(tc.tile_pool(name="op", bufs=3))
         smp = ctx.enter_context(tc.tile_pool(name="smp", bufs=3))
         ps_y = ctx.enter_context(tc.psum_pool(name="ps_y", bufs=2))
         ps_t = ctx.enter_context(tc.psum_pool(name="ps_t", bufs=4))
+
         ps_z = ctx.enter_context(tc.psum_pool(name="ps_z", bufs=2))
 
         w_sb = const.tile([P, E], BF16)
@@ -48,26 +55,34 @@ def tile_linearattention_pb_t_kernel(tc, h_attn, xn, Wout, bout, outnorm_g, out)
 
         loads = []
         for b in range(B):
-            widths = (512, 512, 1024, 2048) if b == 0 else (2048, 2048)
+            widths = (512, 512, 512, 512, 2048) if b == 0 else (2048, 2048)
             n0 = 0
             for wl in widths:
                 loads.append((b, n0, wl))
                 n0 += wl
+        load_chunks = [[(b * N + n0) // CH + k for k in range(wl // CH)] for (b, n0, wl) in loads]
         raw_of = {}
         xn_of = {}
+        state = {"next_load": 0}
 
-        def issue_load(li):
+        def issue_load():
+            li = state["next_load"]
+            state["next_load"] = li + 1
             b, n0, wl = loads[li]
-            raw = rawp.tile([P, PACK, wl], BF16, name="raw", tag="raw")
+            if wl == CH:
+                raw = rawsp.tile([P, PACK, wl], BF16, name="raws", tag="raws")
+            else:
+                raw = rawp.tile([P, PACK, wl], BF16, name="raw", tag="raw")
             src = h_attn[b].rearrange("(p j) h w -> p j (h w)", j=PACK)
             nc.sync.dma_start(out=raw[:], in_=src[:, :, n0:n0 + wl])
-            for k in range(wl // CH):
-                raw_of[(b * N + n0) // CH + k] = (raw, k * CH)
+            for k, c in enumerate(load_chunks[li]):
+                raw_of[c] = (raw, k * CH)
 
         def issue_xn(b):
-            xt = xnp.tile([P, N], BF16, name="xt", tag="xt")
-            nc.sync.dma_start(out=xt[:], in_=xn[b].rearrange("c h w -> c (h w)"))
-            xn_of[b] = xt
+            if b < B and b not in xn_of:
+                xt = xnp.tile([P, N], BF16, name="xt", tag="xt")
+                nc.sync.dma_start(out=xt[:], in_=xn[b].rearrange("c h w -> c (h w)"))
+                xn_of[b] = xt
 
         eps_col = const.tile([P, 1], F32)
         nc.vector.memset(eps_col[:], EPS)
@@ -78,12 +93,11 @@ def tile_linearattention_pb_t_kernel(tc, h_attn, xn, Wout, bout, outnorm_g, out)
         ident_f = const.tile([P, P], F32)
         make_identity(nc, ident_f[:])
 
-        issue_load(0)
-        issue_load(1)
-        issue_load(2)
+        for li in range(5):
+            issue_load()
         issue_xn(0)
-        issue_load(3)
-        next_load = 4
+        for li in range(3):
+            issue_load()
 
         w_r = const.tile([P, PACK, P], BF16)
         nc.vector.tensor_copy(out=w_r[:], in_=w_sb[:].rearrange("c (p t) -> c t p", t=PACK))
@@ -116,44 +130,105 @@ def tile_linearattention_pb_t_kernel(tc, h_attn, xn, Wout, bout, outnorm_g, out)
                 store_of[(b * N + n0) // CH + k] = (si, k * CH, k == wl // CH - 1)
         o_tiles = {}
 
-        n_chunks = B * N // CH
-        for pair in range(n_chunks // 2):
-            chunks = (2 * pair, 2 * pair + 1)
-            st = smp.tile([P, 2 * NBLK, 6], F32, name="st", tag="st")
-            tTs = []
-            for ci, c in enumerate(chunks):
-                if c not in raw_of:
-                    issue_load(next_load)
-                    next_load += 1
-                b = c * CH // N
-                if b not in xn_of:
-                    issue_xn(b)
-                raw, off = raw_of[c]
-                g = grp.tile([P, CH, PACK], BF16, name="g", tag="g", align_bytes=64)
-                dst = g[:].rearrange("p (c i) t -> p c t i", i=4)
-                src = raw[:, :, off:off + CH].rearrange("p t (c i) -> p c t i", i=4)
-                if c in S_REGROUP:
-                    nc.scalar.copy(out=dst, in_=src)
-                else:
-                    nc.vector.tensor_copy(out=dst, in_=src)
-                codes = cdp.tile([P, CH], U32, name="codes", tag="codes", align_bytes=64)
-                scales = cdp.tile([P, CH], U8, name="scales", tag="scales", align_bytes=64)
-                nc.vector.quantize_mx(out=codes[:].bitcast(FP8X4), scales=scales[:],
-                                      in_=g[:].rearrange("p w t -> p (w t)"))
-                y = ps_y.tile([P, CH], F32, name="y", tag="y")
-                nc.tensor.matmul_mx(out=y[:], lhsT=w_codes[:].bitcast(FP8X4), lhsT_scale=w_scales[:],
-                                    rhs=codes[:].bitcast(FP8X4), rhs_scale=scales[:],
-                                    start=True, stop=True)
-                t = tp.tile([P, CH], F32, name="t", tag="t")
-                nc.scalar.activation(out=t[:], in_=y[:], func=ACT.Identity, bias=b_col, scale=1.0)
-                tT = ps_t.tile([P, NBLK, P], F32, name="tT", tag="tT")
-                for k in range(NBLK):
-                    nc.tensor.transpose(tT[:, k, :], t[:, k * P:(k + 1) * P], ident_f[:])
-                for k in range(NBLK):
-                    nc.vector.bn_stats(out=st[:, ci * NBLK + k, :], in_=tT[:, k, :])
-                tTs.append(tT)
+        g_of, r_done, cs_of, y_of, t_of, tT_of, tU_of, z_of, zT_of = {}, {}, {}, {}, {}, {}, {}, {}, {}
+        st_of, sm_of, sd_of, rs_of = {}, {}, {}, {}
+        GS = 1
+        nb = 2 * NBLK * GS
 
-            nb = 2 * NBLK
+        def ok(c):
+            return 0 <= c < NCH
+
+        def who(c):
+            pl = HEAD[c // 2] if c // 2 < len(HEAD) else STEADY
+            return pl[c % 2]
+
+        def regroup(c, eng, q0, nq):
+            if c not in g_of:
+                g_of[c] = grp.tile([P, CH, PACK], BF16, name="g%s" % (c % 2), tag="g%s" % (c % 2), align_bytes=64)
+                r_done[c] = 0
+            raw, off = raw_of[c]
+            dst = g_of[c][:].rearrange("p (c i) t -> p c t i", i=4)[:, q0 * 32:(q0 + nq) * 32]
+            src = raw[:, :, off:off + CH].rearrange("p t (c i) -> p c t i", i=4)[:, q0 * 32:(q0 + nq) * 32]
+            if eng == "V":
+                nc.vector.tensor_copy(out=dst, in_=src)
+            elif eng == "S":
+                nc.scalar.copy(out=dst, in_=src)
+            else:
+                nc.gpsimd.tensor_scalar(out=dst, in0=src, scalar1=1.0, scalar2=0.0, op0=ALU.mult, op1=ALU.add)
+            r_done[c] += nq
+            while state["next_load"] < len(loads):
+                old = state["next_load"] - 4
+                if all(r_done.get(x, 0) == 4 for x in load_chunks[old]):
+                    issue_load()
+                else:
+                    break
+
+        def regroup_whole(eng, p):
+            for c in (2 * p, 2 * p + 1):
+                if ok(c) and who(c) == eng:
+                    regroup(c, eng, 0, 4)
+
+        def regroup_piece(pieces):
+            if pieces:
+                c, q = pieces.pop(0)
+                regroup(c, "S", q, 1)
+
+        def quant(c):
+            if not ok(c):
+                return
+            codes = cdp.tile([P, CH], U32, name="codes", tag="codes", align_bytes=64)
+            scales = cdp.tile([P, CH], U8, name="scales", tag="scales", align_bytes=64)
+            nc.vector.quantize_mx(out=codes[:].bitcast(FP8X4), scales=scales[:],
+                                  in_=g_of[c][:].rearrange("p w t -> p (w t)"))
+            cs_of[c] = (codes, scales)
+
+        def mx(c):
+            if not ok(c):
+                return
+            codes, scales = cs_of[c]
+            y = ps_y.tile([P, CH], F32, name="y", tag="y")
+            nc.tensor.matmul_mx(out=y[:], lhsT=w_codes[:].bitcast(FP8X4), lhsT_scale=w_scales[:],
+                                rhs=codes[:].bitcast(FP8X4), rhs_scale=scales[:], start=True, stop=True)
+            y_of[c] = y
+
+        def bias(c):
+            if not ok(c):
+                return
+            t = tp.tile([P, CH], F32, name="t", tag="t")
+            nc.scalar.activation(out=t[:], in_=y_of[c][:], func=ACT.Identity, bias=b_col, scale=1.0)
+            t_of[c] = t
+
+        def fwd(c):
+            if not ok(c):
+                return
+            tT = ps_t.tile([P, NBLK, P], F32, name="tT", tag="tT")
+            for k in range(NBLK):
+                nc.tensor.transpose(tT[:, k, :], t_of[c][:, k * P:(k + 1) * P], ident_f[:])
+            tT_of[c] = tT
+            tU_of[c] = tT
+
+        def fwd2(c):
+            if not ok(c):
+                return
+            tU = ps_t.tile([P, NBLK, P], F32, name="tU", tag="tU")
+            for k in range(NBLK):
+                nc.tensor.transpose(tU[:, k, :], t_of[c][:, k * P:(k + 1) * P], ident_f[:])
+            tU_of[c] = tU
+
+        def stats(c):
+            if not ok(c):
+                return
+            gi = c // (2 * GS)
+            if gi not in st_of:
+                st_of[gi] = smp.tile([P, nb, 6], F32, name="st", tag="st")
+            for k in range(NBLK):
+                nc.vector.bn_stats(out=st_of[gi][:, (c % (2 * GS)) * NBLK + k, :], in_=tT_of[c][:, k, :])
+
+        def small1(p):
+            if not (0 <= p < NPAIR) or p % GS != GS - 1:
+                return
+            gi = p // GS
+            st = st_of[gi]
             sm = smp.tile([P, nb, 3], F32, name="sm", tag="sm")
             nc.vector.tensor_reduce(out=sm[:], in_=st[:].rearrange("p b (h s) -> p b s h", h=2),
                                     axis=AX.X, op=ALU.add)
@@ -166,31 +241,87 @@ def tile_linearattention_pb_t_kernel(tc, h_attn, xn, Wout, bout, outnorm_g, out)
                                            op0=ALU.mult, op1=ALU.add)
             sd = smp.tile([P, nb], F32, name="sd", tag="sd")
             nc.scalar.activation(out=sd[:], in_=v[:], func=ACT.Sqrt, bias=eps_col[:], scale=1.0 / C)
-            rstd = smp.tile([P, nb], F32, name="rstd", tag="rstd")
-            nc.vector.reciprocal(out=rstd[:], in_=sd[:])
-            nmr = smp.tile([P, nb], F32, name="nmr", tag="nmr")
-            nc.vector.scalar_tensor_tensor(out=nmr[:], in0=sm[:, :, 1], scalar=-0.5, in1=rstd[:],
-                                           op0=ALU.mult, op1=ALU.mult)
+            sm_of[gi] = sm
+            sd_of[gi] = sd
 
-            for ci, c in enumerate(chunks):
-                b = c * CH // N
-                tT = tTs[ci]
-                z = zp.tile([P, NBLK, P], F32, name="z", tag="z")
-                for k in range(NBLK):
-                    j = ci * NBLK + k
-                    nc.scalar.activation(out=z[:, k, :], in_=tT[:, k, :], func=ACT.Identity,
+        def small2(p):
+            if not (0 <= p < NPAIR) or p % GS != GS - 1:
+                return
+            gi = p // GS
+            rstd = smp.tile([P, nb], F32, name="rstd", tag="rstd")
+            nc.vector.reciprocal(out=rstd[:], in_=sd_of[gi][:])
+            nmr = smp.tile([P, nb], F32, name="nmr", tag="nmr")
+            nc.vector.scalar_tensor_tensor(out=nmr[:], in0=sm_of[gi][:, :, 1], scalar=-0.5, in1=rstd[:],
+                                           op0=ALU.mult, op1=ALU.mult)
+            rs_of[gi] = (rstd, nmr)
+
+        def norm(c, eng):
+            if not ok(c) or (c in NV_CHUNKS) != (eng == "V"):
+                return
+            rstd, nmr = rs_of[c // (2 * GS)]
+            z = zp.tile([P, NBLK, P], F32, name="z", tag="z")
+            for k in range(NBLK):
+                j = (c % (2 * GS)) * NBLK + k
+                if eng == "S":
+                    nc.scalar.activation(out=z[:, k, :], in_=tU_of[c][:, k, :], func=ACT.Identity,
                                          bias=nmr[:, j:j + 1], scale=rstd[:, j:j + 1])
-                zT = ps_z.tile([P, CH], F32, name="zT", tag="zT")
-                for k in range(NBLK):
-                    nc.tensor.transpose(zT[:, k * P:(k + 1) * P], z[:, k, :], ident_f[:])
-                si, ooff, last = store_of[c]
-                sb, sn0, swl = stores[si]
-                if si not in o_tiles:
-                    o_tiles[si] = op.tile([P, swl], F32, name="o", tag="o")
-                o = o_tiles[si]
-                n_in_img = c * CH - b * N
-                nc.vector.scalar_tensor_tensor(out=o[:, ooff:ooff + CH], in0=zT[:], scalar=g_col,
-                                               in1=xn_of[b][:, n_in_img:n_in_img + CH],
-                                               op0=ALU.mult, op1=ALU.add)
-                if last:
-                    nc.sync.dma_start(out=out[sb].rearrange("c h w -> c (h w)")[:, sn0:sn0 + swl], in_=o[:])
+                else:
+                    nc.vector.tensor_scalar(out=z[:, k, :], in0=tU_of[c][:, k, :], scalar1=rstd[:, j:j + 1],
+                                            scalar2=nmr[:, j:j + 1], op0=ALU.mult, op1=ALU.add)
+            z_of[c] = z
+
+        def norm_s(c):
+            norm(c, "S")
+
+        def norm_v(c):
+            norm(c, "V")
+
+        def back(c):
+            if not ok(c):
+                return
+            zT = ps_z.tile([P, CH], F32, name="zT", tag="zT")
+            for k in range(NBLK):
+                nc.tensor.transpose(zT[:, k * P:(k + 1) * P], z_of[c][:, k, :], ident_f[:])
+            zT_of[c] = zT
+
+        def final(c):
+            if not ok(c):
+                return
+            b = c * CH // N
+            si, ooff, last = store_of[c]
+            sb, sn0, swl = stores[si]
+            if si not in o_tiles:
+                o_tiles[si] = op.tile([P, swl], F32, name="o", tag="o")
+            o = o_tiles[si]
+            n_in_img = c * CH - b * N
+            nc.vector.scalar_tensor_tensor(out=o[:, ooff:ooff + CH], in0=zT_of[c][:], scalar=g_col,
+                                           in1=xn_of[b][:, n_in_img:n_in_img + CH], op0=ALU.mult, op1=ALU.add)
+            if last:
+                nc.sync.dma_start(out=out[sb].rearrange("c h w -> c (h w)")[:, sn0:sn0 + swl], in_=o[:])
+
+        for p in range(-6, NPAIR + 6):
+            s_pieces = [(c, q) for c in (2 * (p + LR), 2 * (p + LR) + 1) if ok(c) and who(c) == "S" for q in range(4)]
+            small1(p + 0)
+            regroup_whole("V", p + LR)
+            quant(2 * (p + 3))
+            regroup_piece(s_pieces)
+            small2(p + 0)
+            quant(2 * (p + 3) + 1)
+            mx(2 * (p + 2))
+            mx(2 * (p + 2) + 1)
+            norm_s(2 * (p + 0))
+            norm_s(2 * (p + 0) + 1)
+            final(2 * (p + -1))
+            final(2 * (p + -1) + 1)
+            back(2 * (p + 0))
+            back(2 * (p + 0) + 1)
+            bias(2 * (p + 2))
+            fwd(2 * (p + 2))
+            bias(2 * (p + 2) + 1)
+            fwd(2 * (p + 2) + 1)
+            stats(2 * (p + 1))
+            stats(2 * (p + 1) + 1)
+            if (p + 1) % 4 == 0:
+                issue_xn((p + 1) // 4 + 1)
+            while s_pieces:
+                regroup_piece(s_pieces)

@@ -21,7 +21,7 @@ EPS = 1e-5
 FLOPS = 2 * C * E * B * N
 NCH = B * N // CH
 NPAIR = NCH // 2
-LR = 4
+LR = 3
 HEAD = (("V", "V"),)
 STEADY = ("V", "S")
 NV_CHUNKS = ()
@@ -30,13 +30,13 @@ NV_CHUNKS = ()
 def tile_linearattention_pb_t_kernel(tc, h_attn, xn, Wout, bout, outnorm_g, out):
     nc = tc.nc
     with ExitStack() as ctx:
-
+        ctx.enter_context(tc.manual_schedule())
         const = ctx.enter_context(tc.tile_pool(name="const", bufs=1))
         rawsp = ctx.enter_context(tc.tile_pool(name="rawsp", bufs=4))
         rawp = ctx.enter_context(tc.tile_pool(name="rawp", bufs=4))
         xnp = ctx.enter_context(tc.tile_pool(name="xnp", bufs=3))
         grp = ctx.enter_context(tc.tile_pool(name="grp", bufs=2))
-        cdp = ctx.enter_context(tc.tile_pool(name="cdp", bufs=6))
+        cdp = ctx.enter_context(tc.tile_pool(name="cdp", bufs=4))
         tp = ctx.enter_context(tc.tile_pool(name="tp", bufs=4))
         zp = ctx.enter_context(tc.tile_pool(name="zp", bufs=4))
         op = ctx.enter_context(tc.tile_pool(name="op", bufs=3))
@@ -299,28 +299,31 @@ def tile_linearattention_pb_t_kernel(tc, h_attn, xn, Wout, bout, outnorm_g, out)
             if last:
                 nc.sync.dma_start(out=out[sb].rearrange("c h w -> c (h w)")[:, sn0:sn0 + swl], in_=o[:])
 
-        for p in range(-6, NPAIR + 6):
+        for p in range(-4, NPAIR + 3):
             s_pieces = [(c, q) for c in (2 * (p + LR), 2 * (p + LR) + 1) if ok(c) and who(c) == "S" for q in range(4)]
+            norm_s(2 * (p + -1))
+            norm_s(2 * (p + -1) + 1)
+            back(2 * (p + -1))
+            back(2 * (p + -1) + 1)
+            bias(2 * (p + 1))
+            bias(2 * (p + 1) + 1)
+            fwd(2 * (p + 1))
+            fwd(2 * (p + 1) + 1)
+            stats(2 * (p + 0))
+            stats(2 * (p + 0) + 1)
             small1(p + 0)
-            regroup_whole("V", p + LR)
-            quant(2 * (p + 3))
-            regroup_piece(s_pieces)
-            small2(p + 0)
-            quant(2 * (p + 3) + 1)
+            quant(2 * (p + 2))
+            quant(2 * (p + 2) + 1)
             mx(2 * (p + 2))
             mx(2 * (p + 2) + 1)
-            norm_s(2 * (p + 0))
-            norm_s(2 * (p + 0) + 1)
+            regroup_whole("V", p + LR)
+            regroup_piece(s_pieces)
+            regroup_piece(s_pieces)
+            regroup_piece(s_pieces)
+            regroup_piece(s_pieces)
+            small2(p + 0)
             final(2 * (p + -1))
             final(2 * (p + -1) + 1)
-            back(2 * (p + 0))
-            back(2 * (p + 0) + 1)
-            bias(2 * (p + 2))
-            fwd(2 * (p + 2))
-            bias(2 * (p + 2) + 1)
-            fwd(2 * (p + 2) + 1)
-            stats(2 * (p + 1))
-            stats(2 * (p + 1) + 1)
             if (p + 1) % 4 == 0:
                 issue_xn((p + 1) // 4 + 1)
             while s_pieces:

@@ -21,7 +21,7 @@ EPS = 1e-5
 FLOPS = 2 * C * E * B * N
 NCH = B * N // CH
 NPAIR = NCH // 2
-LR = 3
+LR = 4
 HEAD = (("V", "V"),)
 STEADY = ("V", "S")
 NV_CHUNKS = ()
@@ -30,20 +30,20 @@ NV_CHUNKS = ()
 def tile_linearattention_pb_t_kernel(tc, h_attn, xn, Wout, bout, outnorm_g, out):
     nc = tc.nc
     with ExitStack() as ctx:
-        ctx.enter_context(tc.manual_schedule())
+
         const = ctx.enter_context(tc.tile_pool(name="const", bufs=1))
         rawsp = ctx.enter_context(tc.tile_pool(name="rawsp", bufs=4))
         rawp = ctx.enter_context(tc.tile_pool(name="rawp", bufs=4))
         xnp = ctx.enter_context(tc.tile_pool(name="xnp", bufs=3))
         grp = ctx.enter_context(tc.tile_pool(name="grp", bufs=2))
-        cdp = ctx.enter_context(tc.tile_pool(name="cdp", bufs=4))
-        tp = ctx.enter_context(tc.tile_pool(name="tp", bufs=4))
+        cdp = ctx.enter_context(tc.tile_pool(name="cdp", bufs=6))
+        tp = ctx.enter_context(tc.tile_pool(name="tp", bufs=8))
         zp = ctx.enter_context(tc.tile_pool(name="zp", bufs=4))
         op = ctx.enter_context(tc.tile_pool(name="op", bufs=3))
         smp = ctx.enter_context(tc.tile_pool(name="smp", bufs=3))
         ps_y = ctx.enter_context(tc.psum_pool(name="ps_y", bufs=2))
-        ps_t = ctx.enter_context(tc.psum_pool(name="ps_t", bufs=4))
-
+        ps_t = ctx.enter_context(tc.psum_pool(name="ps_t", bufs=2))
+        ps_u = ctx.enter_context(tc.psum_pool(name="ps_u", bufs=2))
         ps_z = ctx.enter_context(tc.psum_pool(name="ps_z", bufs=2))
 
         w_sb = const.tile([P, E], BF16)
@@ -205,12 +205,12 @@ def tile_linearattention_pb_t_kernel(tc, h_attn, xn, Wout, bout, outnorm_g, out)
             for k in range(NBLK):
                 nc.tensor.transpose(tT[:, k, :], t_of[c][:, k * P:(k + 1) * P], ident_f[:])
             tT_of[c] = tT
-            tU_of[c] = tT
+
 
         def fwd2(c):
             if not ok(c):
                 return
-            tU = ps_t.tile([P, NBLK, P], F32, name="tU", tag="tU")
+            tU = ps_u.tile([P, NBLK, P], F32, name="tU", tag="tU")
             for k in range(NBLK):
                 nc.tensor.transpose(tU[:, k, :], t_of[c][:, k * P:(k + 1) * P], ident_f[:])
             tU_of[c] = tU
@@ -299,31 +299,30 @@ def tile_linearattention_pb_t_kernel(tc, h_attn, xn, Wout, bout, outnorm_g, out)
             if last:
                 nc.sync.dma_start(out=out[sb].rearrange("c h w -> c (h w)")[:, sn0:sn0 + swl], in_=o[:])
 
-        for p in range(-4, NPAIR + 3):
+        for p in range(-6, NPAIR + 3):
             s_pieces = [(c, q) for c in (2 * (p + LR), 2 * (p + LR) + 1) if ok(c) and who(c) == "S" for q in range(4)]
-            norm_s(2 * (p + -1))
-            norm_s(2 * (p + -1) + 1)
-            back(2 * (p + -1))
-            back(2 * (p + -1) + 1)
-            bias(2 * (p + 1))
-            bias(2 * (p + 1) + 1)
-            fwd(2 * (p + 1))
-            fwd(2 * (p + 1) + 1)
-            stats(2 * (p + 0))
-            stats(2 * (p + 0) + 1)
             small1(p + 0)
-            quant(2 * (p + 2))
-            quant(2 * (p + 2) + 1)
-            mx(2 * (p + 2))
-            mx(2 * (p + 2) + 1)
             regroup_whole("V", p + LR)
-            regroup_piece(s_pieces)
-            regroup_piece(s_pieces)
-            regroup_piece(s_pieces)
+            quant(2 * (p + 3))
             regroup_piece(s_pieces)
             small2(p + 0)
+            quant(2 * (p + 3) + 1)
+            mx(2 * (p + 2))
+            mx(2 * (p + 2) + 1)
+            fwd2(2 * (p + 0))
+            fwd2(2 * (p + 0) + 1)
+            norm_s(2 * (p + 0))
+            norm_s(2 * (p + 0) + 1)
             final(2 * (p + -1))
             final(2 * (p + -1) + 1)
+            back(2 * (p + 0))
+            back(2 * (p + 0) + 1)
+            stats(2 * (p + 1))
+            stats(2 * (p + 1) + 1)
+            bias(2 * (p + 2))
+            fwd(2 * (p + 2))
+            bias(2 * (p + 2) + 1)
+            fwd(2 * (p + 2) + 1)
             if (p + 1) % 4 == 0:
                 issue_xn((p + 1) // 4 + 1)
             while s_pieces:

@@ -37,10 +37,10 @@ def tile_linearattention_pb_t_kernel(tc, h_attn, xn, Wout, bout, outnorm_g, out)
         xnp = ctx.enter_context(tc.tile_pool(name="xnp", bufs=3))
         grp = ctx.enter_context(tc.tile_pool(name="grp", bufs=2))
         cdp = ctx.enter_context(tc.tile_pool(name="cdp", bufs=6))
-        tp = ctx.enter_context(tc.tile_pool(name="tp", bufs=8))
+        tp = ctx.enter_context(tc.tile_pool(name="tp", bufs=10))
         zp = ctx.enter_context(tc.tile_pool(name="zp", bufs=4))
         op = ctx.enter_context(tc.tile_pool(name="op", bufs=3))
-        smp = ctx.enter_context(tc.tile_pool(name="smp", bufs=3))
+        smp = ctx.enter_context(tc.tile_pool(name="smp", bufs=4))
         ps_y = ctx.enter_context(tc.psum_pool(name="ps_y", bufs=2))
         ps_t = ctx.enter_context(tc.psum_pool(name="ps_t", bufs=2))
         ps_u = ctx.enter_context(tc.psum_pool(name="ps_u", bufs=2))
@@ -87,7 +87,7 @@ def tile_linearattention_pb_t_kernel(tc, h_attn, xn, Wout, bout, outnorm_g, out)
         eps_col = const.tile([P, 1], F32)
         nc.vector.memset(eps_col[:], EPS)
         junk = const.tile([P, 1], F32)
-        nc.scalar.activation(out=junk[:], in_=eps_col[:], func=ACT.Sqrt)
+        nc.scalar.activation(out=junk[:], in_=eps_col[:], func=ACT.Abs_reciprocal_sqrt)
         ident_b = const.tile([P, P], BF16)
         make_identity(nc, ident_b[:])
         ident_f = const.tile([P, P], F32)
@@ -229,31 +229,32 @@ def tile_linearattention_pb_t_kernel(tc, h_attn, xn, Wout, bout, outnorm_g, out)
                 return
             gi = p // GS
             st = st_of[gi]
-            sm = smp.tile([P, nb, 3], F32, name="sm", tag="sm")
-            nc.vector.tensor_reduce(out=sm[:], in_=st[:].rearrange("p b (h s) -> p b s h", h=2),
-                                    axis=AX.X, op=ALU.add)
             d = smp.tile([P, nb], F32, name="d", tag="d")
-            nc.vector.tensor_tensor(out=d[:], in0=st[:, :, 1], in1=st[:, :, 4], op=ALU.subtract)
+            nc.gpsimd.tensor_tensor(out=d[:], in0=st[:, :, 1], in1=st[:, :, 4], op=ALU.subtract)
+            d32 = smp.tile([P, nb], F32, name="d32", tag="d32")
+            nc.gpsimd.tensor_scalar(out=d32[:], in0=d[:], scalar1=float(C) / 4.0, scalar2=0.0, op0=ALU.mult, op1=ALU.add)
+            m2 = smp.tile([P, nb], F32, name="m2", tag="m2")
+            nc.gpsimd.tensor_tensor(out=m2[:], in0=st[:, :, 2], in1=st[:, :, 5], op=ALU.add)
             dd = smp.tile([P, nb], F32, name="dd", tag="dd")
-            nc.vector.tensor_tensor(out=dd[:], in0=d[:], in1=d[:], op=ALU.mult)
+            nc.gpsimd.tensor_tensor(out=dd[:], in0=d32[:], in1=d[:], op=ALU.mult)
             v = smp.tile([P, nb], F32, name="v", tag="v")
-            nc.vector.scalar_tensor_tensor(out=v[:], in0=dd[:], scalar=float(C) / 4.0, in1=sm[:, :, 2],
-                                           op0=ALU.mult, op1=ALU.add)
-            sd = smp.tile([P, nb], F32, name="sd", tag="sd")
-            nc.scalar.activation(out=sd[:], in_=v[:], func=ACT.Sqrt, bias=eps_col[:], scale=1.0 / C)
-            sm_of[gi] = sm
-            sd_of[gi] = sd
+            nc.gpsimd.tensor_tensor(out=v[:], in0=dd[:], in1=m2[:], op=ALU.add)
+            rstd = smp.tile([P, nb], F32, name="rstd", tag="rstd")
+            nc.scalar.activation(out=rstd[:], in_=v[:], func=ACT.Abs_reciprocal_sqrt, bias=eps_col[:], scale=1.0 / C)
+            s = smp.tile([P, nb], F32, name="s", tag="s")
+            nc.gpsimd.tensor_tensor(out=s[:], in0=st[:, :, 1], in1=st[:, :, 4], op=ALU.add)
+            sneg = smp.tile([P, nb], F32, name="sneg", tag="sneg")
+            nc.gpsimd.tensor_scalar(out=sneg[:], in0=s[:], scalar1=-0.5, scalar2=0.0, op0=ALU.mult, op1=ALU.add)
+            sm_of[gi] = sneg
+            sd_of[gi] = rstd
 
         def small2(p):
             if not (0 <= p < NPAIR) or p % GS != GS - 1:
                 return
             gi = p // GS
-            rstd = smp.tile([P, nb], F32, name="rstd", tag="rstd")
-            nc.vector.reciprocal(out=rstd[:], in_=sd_of[gi][:])
             nmr = smp.tile([P, nb], F32, name="nmr", tag="nmr")
-            nc.vector.scalar_tensor_tensor(out=nmr[:], in0=sm_of[gi][:, :, 1], scalar=-0.5, in1=rstd[:],
-                                           op0=ALU.mult, op1=ALU.mult)
-            rs_of[gi] = (rstd, nmr)
+            nc.gpsimd.tensor_tensor(out=nmr[:], in0=sm_of[gi][:], in1=sd_of[gi][:], op=ALU.mult)
+            rs_of[gi] = (sd_of[gi], nmr)
 
         def norm(c, eng):
             if not ok(c) or (c in NV_CHUNKS) != (eng == "V"):
@@ -299,7 +300,7 @@ def tile_linearattention_pb_t_kernel(tc, h_attn, xn, Wout, bout, outnorm_g, out)
             if last:
                 nc.sync.dma_start(out=out[sb].rearrange("c h w -> c (h w)")[:, sn0:sn0 + swl], in_=o[:])
 
-        for p in range(-6, NPAIR + 3):
+        for p in range(-6, NPAIR + 4):
             s_pieces = [(c, q) for c in (2 * (p + LR), 2 * (p + LR) + 1) if ok(c) and who(c) == "S" for q in range(4)]
             small1(p + 0)
             regroup_whole("V", p + LR)
@@ -309,14 +310,14 @@ def tile_linearattention_pb_t_kernel(tc, h_attn, xn, Wout, bout, outnorm_g, out)
             quant(2 * (p + 3) + 1)
             mx(2 * (p + 2))
             mx(2 * (p + 2) + 1)
-            fwd2(2 * (p + 0))
-            fwd2(2 * (p + 0) + 1)
-            norm_s(2 * (p + 0))
-            norm_s(2 * (p + 0) + 1)
-            final(2 * (p + -1))
-            final(2 * (p + -1) + 1)
-            back(2 * (p + 0))
-            back(2 * (p + 0) + 1)
+            fwd2(2 * (p + -1))
+            fwd2(2 * (p + -1) + 1)
+            norm_s(2 * (p + -1))
+            norm_s(2 * (p + -1) + 1)
+            final(2 * (p + -2))
+            final(2 * (p + -2) + 1)
+            back(2 * (p + -1))
+            back(2 * (p + -1) + 1)
             stats(2 * (p + 1))
             stats(2 * (p + 1) + 1)
             bias(2 * (p + 2))

@@ -13,318 +13,266 @@ ACT = mybir.ActivationFunctionType
 AX = mybir.AxisListType
 
 P = 128
-B, C, E, N = 4, 128, 512, 4096
+IMAGES, C, K, N = 4, 128, 512, 4096
 PACK = 4
-CH = 512
-NBLK = CH // P
+CHUNK = 512
+BLOCKS = CHUNK // P
+QUARTER = CHUNK // 4
+N_CHUNKS = IMAGES * N // CHUNK
+N_PAIRS = N_CHUNKS // 2
+PAIR_BLOCKS = 2 * BLOCKS
 EPS = 1e-5
-FLOPS = 2 * C * E * B * N
-NCH = B * N // CH
-NPAIR = NCH // 2
-LR = 4
-HEAD = (("V", "V"),)
-STEADY = ("V", "S")
-NV_CHUNKS = ()
+FLOPS = 2 * C * K * IMAGES * N
+
+AHEAD_REGROUP = 4
+AHEAD_QUANTISE = 3
+AHEAD_MULTIPLY = 2
+AHEAD_STATS = 1
+BIG_LOAD = 2048
+RAW_SLOTS = 4
 
 
 def tile_linearattention_pb_t_kernel(tc, h_attn, xn, Wout, bout, outnorm_g, out):
     nc = tc.nc
     with ExitStack() as ctx:
-
         const = ctx.enter_context(tc.tile_pool(name="const", bufs=1))
-        rawsp = ctx.enter_context(tc.tile_pool(name="rawsp", bufs=4))
-        rawp = ctx.enter_context(tc.tile_pool(name="rawp", bufs=4))
-        xnp = ctx.enter_context(tc.tile_pool(name="xnp", bufs=3))
-        grp = ctx.enter_context(tc.tile_pool(name="grp", bufs=2))
-        cdp = ctx.enter_context(tc.tile_pool(name="cdp", bufs=6))
-        tp = ctx.enter_context(tc.tile_pool(name="tp", bufs=10))
-        zp = ctx.enter_context(tc.tile_pool(name="zp", bufs=4))
-        op = ctx.enter_context(tc.tile_pool(name="op", bufs=3))
-        smp = ctx.enter_context(tc.tile_pool(name="smp", bufs=4))
-        ps_y = ctx.enter_context(tc.psum_pool(name="ps_y", bufs=2))
-        ps_t = ctx.enter_context(tc.psum_pool(name="ps_t", bufs=2))
-        ps_u = ctx.enter_context(tc.psum_pool(name="ps_u", bufs=2))
-        ps_z = ctx.enter_context(tc.psum_pool(name="ps_z", bufs=2))
+        raw_small = ctx.enter_context(tc.tile_pool(name="raw_small", bufs=4))
+        raw_big = ctx.enter_context(tc.tile_pool(name="raw_big", bufs=RAW_SLOTS))
+        resid = ctx.enter_context(tc.tile_pool(name="resid", bufs=3))
+        grouped = ctx.enter_context(tc.tile_pool(name="grouped", bufs=2))
+        quantised = ctx.enter_context(tc.tile_pool(name="quantised", bufs=2 * AHEAD_QUANTISE))
+        biased = ctx.enter_context(tc.tile_pool(name="biased", bufs=4))
+        normed = ctx.enter_context(tc.tile_pool(name="normed", bufs=4))
+        result = ctx.enter_context(tc.tile_pool(name="result", bufs=3))
+        small = ctx.enter_context(tc.tile_pool(name="small", bufs=3))
+        psum_y = ctx.enter_context(tc.psum_pool(name="psum_y", bufs=2))
+        psum_fwd = ctx.enter_context(tc.psum_pool(name="psum_fwd", bufs=4))
+        psum_back = ctx.enter_context(tc.psum_pool(name="psum_back", bufs=2))
 
-        w_sb = const.tile([P, E], BF16)
+        w_sb = const.tile([P, K], BF16)
         nc.scalar.dma_start(out=w_sb[:], in_=Wout)
-        bg = const.tile([P, P], BF16)
-        nc.vector.memset(bg[:], 0.0)
-        nc.scalar.dma_start(out=bg[0:1, :], in_=bout.unsqueeze(0))
-        nc.scalar.dma_start(out=bg[1:2, :], in_=outnorm_g.rearrange("a c h w -> (a h w) c"))
+        vec_rows = const.tile([P, P], BF16)
+        nc.vector.memset(vec_rows[:], 0.0)
+        nc.scalar.dma_start(out=vec_rows[0:1, :], in_=bout.unsqueeze(0))
+        nc.scalar.dma_start(out=vec_rows[1:2, :], in_=outnorm_g.rearrange("a c h w -> (a h w) c"))
 
         loads = []
-        for b in range(B):
-            widths = (512, 512, 512, 512, 2048) if b == 0 else (2048, 2048)
+        for b in range(IMAGES):
+            widths = (CHUNK,) * 4 + (BIG_LOAD,) if b == 0 else (BIG_LOAD,) * 2
             n0 = 0
-            for wl in widths:
-                loads.append((b, n0, wl))
-                n0 += wl
-        load_chunks = [[(b * N + n0) // CH + k for k in range(wl // CH)] for (b, n0, wl) in loads]
+            for width in widths:
+                loads.append((b, n0, width))
+                n0 += width
+        chunks_of_load = [[(b * N + n0) // CHUNK + j for j in range(width // CHUNK)] for (b, n0, width) in loads]
         raw_of = {}
-        xn_of = {}
-        state = {"next_load": 0}
+        quarters_done = {}
+        resid_of = {}
+        issued = []
 
-        def issue_load():
-            li = state["next_load"]
-            state["next_load"] = li + 1
-            b, n0, wl = loads[li]
-            if wl == CH:
-                raw = rawsp.tile([P, PACK, wl], BF16, name="raws", tag="raws")
+        def load_next():
+            b, n0, width = loads[len(issued)]
+            if width == CHUNK:
+                raw = raw_small.tile([P, PACK, width], BF16, name="raw_s", tag="raw_s")
             else:
-                raw = rawp.tile([P, PACK, wl], BF16, name="raw", tag="raw")
-            src = h_attn[b].rearrange("(p j) h w -> p j (h w)", j=PACK)
-            nc.sync.dma_start(out=raw[:], in_=src[:, :, n0:n0 + wl])
-            for k, c in enumerate(load_chunks[li]):
-                raw_of[c] = (raw, k * CH)
+                raw = raw_big.tile([P, PACK, width], BF16, name="raw_b", tag="raw_b")
+            rows = h_attn[b].rearrange("(p t) h w -> p t (h w)", t=PACK)
+            nc.sync.dma_start(out=raw[:], in_=rows[:, :, n0:n0 + width])
+            for j, c in enumerate(chunks_of_load[len(issued)]):
+                raw_of[c] = (raw, j * CHUNK)
+            issued.append(raw)
 
-        def issue_xn(b):
-            if b < B and b not in xn_of:
-                xt = xnp.tile([P, N], BF16, name="xt", tag="xt")
+        def load_residual(b):
+            if b < IMAGES:
+                xt = resid.tile([P, N], BF16, name="xt", tag="xt")
                 nc.sync.dma_start(out=xt[:], in_=xn[b].rearrange("c h w -> c (h w)"))
-                xn_of[b] = xt
+                resid_of[b] = xt
 
         eps_col = const.tile([P, 1], F32)
         nc.vector.memset(eps_col[:], EPS)
-        junk = const.tile([P, 1], F32)
-        nc.scalar.activation(out=junk[:], in_=eps_col[:], func=ACT.Abs_reciprocal_sqrt)
+        warm = const.tile([P, 1], F32)
+        nc.scalar.activation(out=warm[:], in_=eps_col[:], func=ACT.Abs_reciprocal_sqrt)
         ident_b = const.tile([P, P], BF16)
         make_identity(nc, ident_b[:])
         ident_f = const.tile([P, P], F32)
         make_identity(nc, ident_f[:])
 
-        for li in range(5):
-            issue_load()
-        issue_xn(0)
-        for li in range(3):
-            issue_load()
+        while len(issued) < len(loads) and loads[len(issued)][0] == 0:
+            load_next()
+        load_residual(0)
+        for i in range(RAW_SLOTS - 1):
+            load_next()
 
-        w_r = const.tile([P, PACK, P], BF16)
-        nc.vector.tensor_copy(out=w_r[:], in_=w_sb[:].rearrange("c (p t) -> c t p", t=PACK))
-        w_ps = ps_z.tile([P, PACK, P], BF16, name="w_ps", tag="zT")
+        w_split = const.tile([P, PACK, P], BF16)
+        nc.vector.tensor_copy(out=w_split[:], in_=w_sb[:].rearrange("c (p t) -> c t p", t=PACK))
+        w_ps = psum_back.tile([P, PACK, P], BF16, name="w_ps", tag="back")
         for t in range(PACK):
-            nc.tensor.transpose(w_ps[:, t, :], w_r[:, t, :], ident_b[:])
-        w_g = const.tile([P, P, PACK], BF16, align_bytes=64)
-        nc.vector.tensor_copy(out=w_g[:], in_=w_ps[:].rearrange("p t c -> p c t"))
-        w_codes = const.tile([P, P], U32, align_bytes=64)
-        w_scales = const.tile([P, P], U8, align_bytes=64)
-        nc.vector.quantize_mx(out=w_codes[:].bitcast(FP8X4), scales=w_scales[:],
-                              in_=w_g[:].rearrange("p c t -> p (c t)"))
-        bg_ps = ps_z.tile([P, P], BF16, name="bg_ps", tag="zT")
-        nc.tensor.transpose(bg_ps[:], bg[:], ident_b[:])
-        bgf = const.tile([P, 2], F32)
-        nc.vector.tensor_copy(out=bgf[:], in_=bg_ps[:, 0:2])
-        b_col = bgf[:, 0:1]
-        g_col = bgf[:, 1:2]
+            nc.tensor.transpose(w_ps[:, t, :], w_split[:, t, :], ident_b[:])
+        w_grouped = const.tile([P, C, PACK], BF16, align_bytes=64)
+        nc.vector.tensor_copy(out=w_grouped[:], in_=w_ps[:].rearrange("p t c -> p c t"))
+        w_words = const.tile([P, C], U32, align_bytes=64)
+        w_scales = const.tile([P, C], U8, align_bytes=64)
+        nc.vector.quantize_mx(out=w_words[:].bitcast(FP8X4), scales=w_scales[:],
+                              in_=w_grouped[:].rearrange("p c t -> p (c t)"))
+        vec_ps = psum_back.tile([P, P], BF16, name="vec_ps", tag="back")
+        nc.tensor.transpose(vec_ps[:], vec_rows[:], ident_b[:])
+        vec_cols = const.tile([P, 2], F32)
+        nc.vector.tensor_copy(out=vec_cols[:], in_=vec_ps[:, 0:2])
+        bias_col = vec_cols[:, 0:1]
+        gain_col = vec_cols[:, 1:2]
 
         stores = []
-        for b in range(B):
-            widths = (2048, 1024, 512, 512) if b == B - 1 else (2048, 2048)
+        for b in range(IMAGES):
+            widths = (BIG_LOAD, 2 * CHUNK, CHUNK, CHUNK) if b == IMAGES - 1 else (BIG_LOAD,) * 2
             n0 = 0
-            for wl in widths:
-                stores.append((b, n0, wl))
-                n0 += wl
+            for width in widths:
+                stores.append((b, n0, width))
+                n0 += width
         store_of = {}
-        for si, (b, n0, wl) in enumerate(stores):
-            for k in range(wl // CH):
-                store_of[(b * N + n0) // CH + k] = (si, k * CH, k == wl // CH - 1)
-        o_tiles = {}
+        for s, (b, n0, width) in enumerate(stores):
+            for j in range(width // CHUNK):
+                store_of[(b * N + n0) // CHUNK + j] = (s, j * CHUNK, j == width // CHUNK - 1)
+        result_of = {}
 
-        g_of, r_done, cs_of, y_of, t_of, tT_of, tU_of, z_of, zT_of = {}, {}, {}, {}, {}, {}, {}, {}, {}
-        st_of, sm_of, sd_of, rs_of = {}, {}, {}, {}
-        GS = 1
-        nb = 2 * NBLK * GS
+        grouped_of, words_of, y_of, biased_of, fwd_of, normed_of, back_of = {}, {}, {}, {}, {}, {}, {}
+        stats_of, mean2_of, rstd_of, shift_of = {}, {}, {}, {}
 
-        def ok(c):
-            return 0 <= c < NCH
+        def exists(c):
+            return 0 <= c < N_CHUNKS
 
-        def who(c):
-            pl = HEAD[c // 2] if c // 2 < len(HEAD) else STEADY
-            return pl[c % 2]
+        def regroups_on_vector(c):
+            return c % 2 == 0 or c < 2
 
-        def regroup(c, eng, q0, nq):
-            if c not in g_of:
-                g_of[c] = grp.tile([P, CH, PACK], BF16, name="g%s" % (c % 2), tag="g%s" % (c % 2), align_bytes=64)
-                r_done[c] = 0
-            raw, off = raw_of[c]
-            dst = g_of[c][:].rearrange("p (c i) t -> p c t i", i=4)[:, q0 * 32:(q0 + nq) * 32]
-            src = raw[:, :, off:off + CH].rearrange("p t (c i) -> p c t i", i=4)[:, q0 * 32:(q0 + nq) * 32]
-            if eng == "V":
-                nc.vector.tensor_copy(out=dst, in_=src)
-            elif eng == "S":
-                nc.scalar.copy(out=dst, in_=src)
-            else:
-                nc.gpsimd.tensor_scalar(out=dst, in0=src, scalar1=1.0, scalar2=0.0, op0=ALU.mult, op1=ALU.add)
-            r_done[c] += nq
-            while state["next_load"] < len(loads):
-                old = state["next_load"] - 4
-                if all(r_done.get(x, 0) == 4 for x in load_chunks[old]):
-                    issue_load()
-                else:
-                    break
+        def regroup(c, engine_copy, first_quarter, quarters):
+            if c not in grouped_of:
+                grouped_of[c] = grouped.tile([P, CHUNK, PACK], BF16, name="g%s" % (c % 2), tag="g%s" % (c % 2),
+                                             align_bytes=64)
+                quarters_done[c] = 0
+            raw, col = raw_of[c]
+            runs = slice(first_quarter * QUARTER // 4, (first_quarter + quarters) * QUARTER // 4)
+            engine_copy(out=grouped_of[c][:].rearrange("p (r i) t -> p r t i", i=4)[:, runs],
+                        in_=raw[:, :, col:col + CHUNK].rearrange("p t (r i) -> p r t i", i=4)[:, runs])
+            quarters_done[c] += quarters
+            while len(issued) < len(loads) and all(quarters_done.get(x, 0) == 4
+                                                   for x in chunks_of_load[len(issued) - RAW_SLOTS]):
+                load_next()
 
-        def regroup_whole(eng, p):
-            for c in (2 * p, 2 * p + 1):
-                if ok(c) and who(c) == eng:
-                    regroup(c, eng, 0, 4)
+        def quantise(c):
+            if exists(c):
+                words = quantised.tile([P, CHUNK], U32, name="words", tag="words", align_bytes=64)
+                scales = quantised.tile([P, CHUNK], U8, name="scales", tag="scales", align_bytes=64)
+                nc.vector.quantize_mx(out=words[:].bitcast(FP8X4), scales=scales[:],
+                                      in_=grouped_of[c][:].rearrange("p n t -> p (n t)"))
+                words_of[c] = (words, scales)
 
-        def regroup_piece(pieces):
-            if pieces:
-                c, q = pieces.pop(0)
-                regroup(c, "S", q, 1)
+        def multiply(c):
+            if exists(c):
+                words, scales = words_of[c]
+                y_of[c] = psum_y.tile([P, CHUNK], F32, name="y", tag="y")
+                nc.tensor.matmul_mx(out=y_of[c][:], lhsT=w_words[:].bitcast(FP8X4), lhsT_scale=w_scales[:],
+                                    rhs=words[:].bitcast(FP8X4), rhs_scale=scales[:], start=True, stop=True)
 
-        def quant(c):
-            if not ok(c):
-                return
-            codes = cdp.tile([P, CH], U32, name="codes", tag="codes", align_bytes=64)
-            scales = cdp.tile([P, CH], U8, name="scales", tag="scales", align_bytes=64)
-            nc.vector.quantize_mx(out=codes[:].bitcast(FP8X4), scales=scales[:],
-                                  in_=g_of[c][:].rearrange("p w t -> p (w t)"))
-            cs_of[c] = (codes, scales)
+        def add_bias(c):
+            if exists(c):
+                biased_of[c] = biased.tile([P, CHUNK], F32, name="t", tag="t")
+                nc.scalar.activation(out=biased_of[c][:], in_=y_of[c][:], func=ACT.Identity,
+                                     bias=bias_col, scale=1.0)
 
-        def mx(c):
-            if not ok(c):
-                return
-            codes, scales = cs_of[c]
-            y = ps_y.tile([P, CH], F32, name="y", tag="y")
-            nc.tensor.matmul_mx(out=y[:], lhsT=w_codes[:].bitcast(FP8X4), lhsT_scale=w_scales[:],
-                                rhs=codes[:].bitcast(FP8X4), rhs_scale=scales[:], start=True, stop=True)
-            y_of[c] = y
-
-        def bias(c):
-            if not ok(c):
-                return
-            t = tp.tile([P, CH], F32, name="t", tag="t")
-            nc.scalar.activation(out=t[:], in_=y_of[c][:], func=ACT.Identity, bias=b_col, scale=1.0)
-            t_of[c] = t
-
-        def fwd(c):
-            if not ok(c):
-                return
-            tT = ps_t.tile([P, NBLK, P], F32, name="tT", tag="tT")
-            for k in range(NBLK):
-                nc.tensor.transpose(tT[:, k, :], t_of[c][:, k * P:(k + 1) * P], ident_f[:])
-            tT_of[c] = tT
-
-
-        def fwd2(c):
-            if not ok(c):
-                return
-            tU = ps_u.tile([P, NBLK, P], F32, name="tU", tag="tU")
-            for k in range(NBLK):
-                nc.tensor.transpose(tU[:, k, :], t_of[c][:, k * P:(k + 1) * P], ident_f[:])
-            tU_of[c] = tU
+        def forward(c):
+            if exists(c):
+                fwd_of[c] = psum_fwd.tile([P, BLOCKS, P], F32, name="fwd", tag="fwd")
+                for j in range(BLOCKS):
+                    nc.tensor.transpose(fwd_of[c][:, j, :], biased_of[c][:, j * P:(j + 1) * P], ident_f[:])
 
         def stats(c):
-            if not ok(c):
-                return
-            gi = c // (2 * GS)
-            if gi not in st_of:
-                st_of[gi] = smp.tile([P, nb, 6], F32, name="st", tag="st")
-            for k in range(NBLK):
-                nc.vector.bn_stats(out=st_of[gi][:, (c % (2 * GS)) * NBLK + k, :], in_=tT_of[c][:, k, :])
+            if exists(c):
+                if c // 2 not in stats_of:
+                    stats_of[c // 2] = small.tile([P, PAIR_BLOCKS, 6], F32, name="st", tag="st")
+                for j in range(BLOCKS):
+                    nc.vector.bn_stats(out=stats_of[c // 2][:, (c % 2) * BLOCKS + j, :], in_=fwd_of[c][:, j, :])
 
-        def small1(p):
-            if not (0 <= p < NPAIR) or p % GS != GS - 1:
-                return
-            gi = p // GS
-            st = st_of[gi]
-            d = smp.tile([P, nb], F32, name="d", tag="d")
-            nc.gpsimd.tensor_tensor(out=d[:], in0=st[:, :, 1], in1=st[:, :, 4], op=ALU.subtract)
-            d32 = smp.tile([P, nb], F32, name="d32", tag="d32")
-            nc.gpsimd.tensor_scalar(out=d32[:], in0=d[:], scalar1=float(C) / 4.0, scalar2=0.0, op0=ALU.mult, op1=ALU.add)
-            m2 = smp.tile([P, nb], F32, name="m2", tag="m2")
-            nc.gpsimd.tensor_tensor(out=m2[:], in0=st[:, :, 2], in1=st[:, :, 5], op=ALU.add)
-            dd = smp.tile([P, nb], F32, name="dd", tag="dd")
-            nc.gpsimd.tensor_tensor(out=dd[:], in0=d32[:], in1=d[:], op=ALU.mult)
-            v = smp.tile([P, nb], F32, name="v", tag="v")
-            nc.gpsimd.tensor_tensor(out=v[:], in0=dd[:], in1=m2[:], op=ALU.add)
-            rstd = smp.tile([P, nb], F32, name="rstd", tag="rstd")
-            nc.scalar.activation(out=rstd[:], in_=v[:], func=ACT.Abs_reciprocal_sqrt, bias=eps_col[:], scale=1.0 / C)
-            s = smp.tile([P, nb], F32, name="s", tag="s")
-            nc.gpsimd.tensor_tensor(out=s[:], in0=st[:, :, 1], in1=st[:, :, 4], op=ALU.add)
-            sneg = smp.tile([P, nb], F32, name="sneg", tag="sneg")
-            nc.gpsimd.tensor_scalar(out=sneg[:], in0=s[:], scalar1=-0.5, scalar2=0.0, op0=ALU.mult, op1=ALU.add)
-            sm_of[gi] = sneg
-            sd_of[gi] = rstd
+        def small_first(pair):
+            if 0 <= pair < N_PAIRS:
+                st = stats_of[pair]
+                both = small.tile([P, PAIR_BLOCKS, 3], F32, name="both", tag="both")
+                nc.vector.tensor_reduce(out=both[:], in_=st[:].rearrange("p b (h s) -> p b s h", h=2),
+                                        axis=AX.X, op=ALU.add)
+                d = small.tile([P, PAIR_BLOCKS], F32, name="d", tag="d")
+                nc.vector.tensor_tensor(out=d[:], in0=st[:, :, 1], in1=st[:, :, 4], op=ALU.subtract)
+                dd = small.tile([P, PAIR_BLOCKS], F32, name="dd", tag="dd")
+                nc.vector.tensor_tensor(out=dd[:], in0=d[:], in1=d[:], op=ALU.mult)
+                c_var = small.tile([P, PAIR_BLOCKS], F32, name="c_var", tag="c_var")
+                nc.vector.scalar_tensor_tensor(out=c_var[:], in0=dd[:], scalar=C / 4.0, in1=both[:, :, 2],
+                                               op0=ALU.mult, op1=ALU.add)
+                rstd = small.tile([P, PAIR_BLOCKS], F32, name="rstd", tag="rstd")
+                nc.scalar.activation(out=rstd[:], in_=c_var[:], func=ACT.Abs_reciprocal_sqrt,
+                                     bias=eps_col[:], scale=1.0 / C)
+                mean2_of[pair] = both
+                rstd_of[pair] = rstd
 
-        def small2(p):
-            if not (0 <= p < NPAIR) or p % GS != GS - 1:
-                return
-            gi = p // GS
-            nmr = smp.tile([P, nb], F32, name="nmr", tag="nmr")
-            nc.gpsimd.tensor_tensor(out=nmr[:], in0=sm_of[gi][:], in1=sd_of[gi][:], op=ALU.mult)
-            rs_of[gi] = (sd_of[gi], nmr)
+        def small_second(pair):
+            if 0 <= pair < N_PAIRS:
+                shift_of[pair] = small.tile([P, PAIR_BLOCKS], F32, name="shift", tag="shift")
+                nc.vector.scalar_tensor_tensor(out=shift_of[pair][:], in0=mean2_of[pair][:, :, 1], scalar=-0.5,
+                                               in1=rstd_of[pair][:], op0=ALU.mult, op1=ALU.mult)
 
-        def norm(c, eng):
-            if not ok(c) or (c in NV_CHUNKS) != (eng == "V"):
-                return
-            rstd, nmr = rs_of[c // (2 * GS)]
-            z = zp.tile([P, NBLK, P], F32, name="z", tag="z")
-            for k in range(NBLK):
-                j = (c % (2 * GS)) * NBLK + k
-                if eng == "S":
-                    nc.scalar.activation(out=z[:, k, :], in_=tU_of[c][:, k, :], func=ACT.Identity,
-                                         bias=nmr[:, j:j + 1], scale=rstd[:, j:j + 1])
-                else:
-                    nc.vector.tensor_scalar(out=z[:, k, :], in0=tU_of[c][:, k, :], scalar1=rstd[:, j:j + 1],
-                                            scalar2=nmr[:, j:j + 1], op0=ALU.mult, op1=ALU.add)
-            z_of[c] = z
+        def normalise(c):
+            if exists(c):
+                rstd, shift = rstd_of[c // 2], shift_of[c // 2]
+                normed_of[c] = normed.tile([P, BLOCKS, P], F32, name="z", tag="z")
+                for j in range(BLOCKS):
+                    col = (c % 2) * BLOCKS + j
+                    nc.scalar.activation(out=normed_of[c][:, j, :], in_=fwd_of[c][:, j, :], func=ACT.Identity,
+                                         bias=shift[:, col:col + 1], scale=rstd[:, col:col + 1])
 
-        def norm_s(c):
-            norm(c, "S")
+        def backward(c):
+            if exists(c):
+                back_of[c] = psum_back.tile([P, CHUNK], F32, name="back", tag="back")
+                for j in range(BLOCKS):
+                    nc.tensor.transpose(back_of[c][:, j * P:(j + 1) * P], normed_of[c][:, j, :], ident_f[:])
 
-        def norm_v(c):
-            norm(c, "V")
+        def last(c):
+            if exists(c):
+                s, col, completes = store_of[c]
+                b, n0, width = stores[s]
+                if s not in result_of:
+                    result_of[s] = result.tile([P, width], F32, name="o", tag="o")
+                n = c * CHUNK - b * N
+                nc.vector.scalar_tensor_tensor(out=result_of[s][:, col:col + CHUNK], in0=back_of[c][:],
+                                               scalar=gain_col, in1=resid_of[b][:, n:n + CHUNK],
+                                               op0=ALU.mult, op1=ALU.add)
+                if completes:
+                    nc.sync.dma_start(out=out[b].rearrange("c h w -> c (h w)")[:, n0:n0 + width],
+                                      in_=result_of[s][:])
 
-        def back(c):
-            if not ok(c):
-                return
-            zT = ps_z.tile([P, CH], F32, name="zT", tag="zT")
-            for k in range(NBLK):
-                nc.tensor.transpose(zT[:, k * P:(k + 1) * P], z_of[c][:, k, :], ident_f[:])
-            zT_of[c] = zT
+        for r in range(-AHEAD_REGROUP, N_PAIRS + 1):
+            to_regroup = [c for c in (2 * (r + AHEAD_REGROUP), 2 * (r + AHEAD_REGROUP) + 1) if exists(c)]
+            scalar_quarters = [(c, q) for c in to_regroup if not regroups_on_vector(c) for q in range(4)]
+            even, odd = 2 * r, 2 * r + 1
 
-        def final(c):
-            if not ok(c):
-                return
-            b = c * CH // N
-            si, ooff, last = store_of[c]
-            sb, sn0, swl = stores[si]
-            if si not in o_tiles:
-                o_tiles[si] = op.tile([P, swl], F32, name="o", tag="o")
-            o = o_tiles[si]
-            n_in_img = c * CH - b * N
-            nc.vector.scalar_tensor_tensor(out=o[:, ooff:ooff + CH], in0=zT_of[c][:], scalar=g_col,
-                                           in1=xn_of[b][:, n_in_img:n_in_img + CH], op0=ALU.mult, op1=ALU.add)
-            if last:
-                nc.sync.dma_start(out=out[sb].rearrange("c h w -> c (h w)")[:, sn0:sn0 + swl], in_=o[:])
-
-        for p in range(-6, NPAIR + 4):
-            s_pieces = [(c, q) for c in (2 * (p + LR), 2 * (p + LR) + 1) if ok(c) and who(c) == "S" for q in range(4)]
-            small1(p + 0)
-            regroup_whole("V", p + LR)
-            quant(2 * (p + 3))
-            regroup_piece(s_pieces)
-            small2(p + 0)
-            quant(2 * (p + 3) + 1)
-            mx(2 * (p + 2))
-            mx(2 * (p + 2) + 1)
-            fwd2(2 * (p + -1))
-            fwd2(2 * (p + -1) + 1)
-            norm_s(2 * (p + -1))
-            norm_s(2 * (p + -1) + 1)
-            final(2 * (p + -2))
-            final(2 * (p + -2) + 1)
-            back(2 * (p + -1))
-            back(2 * (p + -1) + 1)
-            stats(2 * (p + 1))
-            stats(2 * (p + 1) + 1)
-            bias(2 * (p + 2))
-            fwd(2 * (p + 2))
-            bias(2 * (p + 2) + 1)
-            fwd(2 * (p + 2) + 1)
-            if (p + 1) % 4 == 0:
-                issue_xn((p + 1) // 4 + 1)
-            while s_pieces:
-                regroup_piece(s_pieces)
+            small_first(r)
+            for c in to_regroup:
+                if regroups_on_vector(c):
+                    regroup(c, nc.vector.tensor_copy, 0, 4)
+            quantise(even + 2 * AHEAD_QUANTISE)
+            for c, q in scalar_quarters[:1]:
+                regroup(c, nc.scalar.copy, q, 1)
+            small_second(r)
+            quantise(odd + 2 * AHEAD_QUANTISE)
+            multiply(even + 2 * AHEAD_MULTIPLY)
+            multiply(odd + 2 * AHEAD_MULTIPLY)
+            normalise(even)
+            normalise(odd)
+            last(even - 2)
+            last(odd - 2)
+            backward(even)
+            backward(odd)
+            add_bias(even + 2 * AHEAD_MULTIPLY)
+            forward(even + 2 * AHEAD_MULTIPLY)
+            add_bias(odd + 2 * AHEAD_MULTIPLY)
+            forward(odd + 2 * AHEAD_MULTIPLY)
+            stats(even + 2 * AHEAD_STATS)
+            stats(odd + 2 * AHEAD_STATS)
+            if (r + 5) % 4 == 0:
+                load_residual((r + 5) // 4)
+            for c, q in scalar_quarters[1:]:
+                regroup(c, nc.scalar.copy, q, 1)

@@ -17,7 +17,8 @@ IMAGES, C, K, N = 4, 128, 512, 4096
 PACK = 4
 CHUNK = 512
 BLOCKS = CHUNK // P
-QUARTER = CHUNK // 4
+EIGHTH = CHUNK // 8
+EIGHTHS = 8
 N_CHUNKS = IMAGES * N // CHUNK
 N_PAIRS = N_CHUNKS // 2
 PAIR_BLOCKS = 2 * BLOCKS
@@ -30,6 +31,11 @@ AHEAD_MULTIPLY = 2
 AHEAD_STATS = 1
 BIG_LOAD = 2048
 RAW_SLOTS = 4
+VECTOR_EIGHTHS = 4
+GPSIMD_EIGHTHS = 7
+GPSIMD_PIECES = (4, 3)
+FIRST_PINNED = 1
+LAST_PINNED = N_PAIRS - 5
 
 
 def tile_linearattention_pb_t_kernel(tc, h_attn, xn, Wout, bout, outnorm_g, out):
@@ -39,7 +45,8 @@ def tile_linearattention_pb_t_kernel(tc, h_attn, xn, Wout, bout, outnorm_g, out)
         raw_small = ctx.enter_context(tc.tile_pool(name="raw_small", bufs=4))
         raw_big = ctx.enter_context(tc.tile_pool(name="raw_big", bufs=RAW_SLOTS))
         resid = ctx.enter_context(tc.tile_pool(name="resid", bufs=3))
-        grouped = ctx.enter_context(tc.tile_pool(name="grouped", bufs=2))
+        grouped_even = ctx.enter_context(tc.tile_pool(name="grouped_even", bufs=2))
+        grouped_odd = ctx.enter_context(tc.tile_pool(name="grouped_odd", bufs=1))
         quantised = ctx.enter_context(tc.tile_pool(name="quantised", bufs=2 * AHEAD_QUANTISE))
         biased = ctx.enter_context(tc.tile_pool(name="biased", bufs=4))
         normed = ctx.enter_context(tc.tile_pool(name="normed", bufs=4))
@@ -65,7 +72,7 @@ def tile_linearattention_pb_t_kernel(tc, h_attn, xn, Wout, bout, outnorm_g, out)
                 n0 += width
         chunks_of_load = [[(b * N + n0) // CHUNK + j for j in range(width // CHUNK)] for (b, n0, width) in loads]
         raw_of = {}
-        quarters_done = {}
+        eighths_done = {}
         resid_of = {}
         issued = []
 
@@ -139,20 +146,38 @@ def tile_linearattention_pb_t_kernel(tc, h_attn, xn, Wout, bout, outnorm_g, out)
         def exists(c):
             return 0 <= c < N_CHUNKS
 
-        def regroups_on_vector(c):
-            return c % 2 == 0 or c < 2
+        def shares(c):
+            if c < 2:
+                return [("vector", 0, EIGHTHS)]
+            if c % 2 == 0:
+                return ([("vector", e, 2) for e in range(0, VECTOR_EIGHTHS, 2)]
+                        + [("scalar", e, 2) for e in range(VECTOR_EIGHTHS, EIGHTHS, 2)])
+            pieces, first = [], 0
+            for width in GPSIMD_PIECES:
+                pieces.append(("gpsimd", first, width))
+                first += width
+            return pieces + [("scalar", first, EIGHTHS - first)]
 
-        def regroup(c, engine_copy, first_quarter, quarters):
+        def regroup(c, engine, first, eighths):
             if c not in grouped_of:
-                grouped_of[c] = grouped.tile([P, CHUNK, PACK], BF16, name="g%s" % (c % 2), tag="g%s" % (c % 2),
-                                             align_bytes=64)
-                quarters_done[c] = 0
+                if c % 2 == 0:
+                    grouped_of[c] = grouped_even.tile([P, CHUNK, PACK], BF16, name="g0", tag="g0", align_bytes=64)
+                else:
+                    grouped_of[c] = grouped_odd.tile([P, CHUNK, PACK], BF16, name="g1", tag="g1", align_bytes=64)
+                eighths_done[c] = 0
             raw, col = raw_of[c]
-            runs = slice(first_quarter * QUARTER // 4, (first_quarter + quarters) * QUARTER // 4)
-            engine_copy(out=grouped_of[c][:].rearrange("p (r i) t -> p r t i", i=4)[:, runs],
-                        in_=raw[:, :, col:col + CHUNK].rearrange("p t (r i) -> p r t i", i=4)[:, runs])
-            quarters_done[c] += quarters
-            while len(issued) < len(loads) and all(quarters_done.get(x, 0) == 4
+            if engine == "gpsimd":
+                n0, n1 = first * EIGHTH, (first + eighths) * EIGHTH
+                nc.gpsimd.tensor_scalar(out=grouped_of[c][:, n0:n1, :],
+                                        in0=raw[:, :, col + n0:col + n1].rearrange("p t n -> p n t"),
+                                        scalar1=1.0, scalar2=0.0, op0=ALU.mult, op1=ALU.add)
+            else:
+                engine_copy = nc.vector.tensor_copy if engine == "vector" else nc.scalar.copy
+                runs = slice(first * EIGHTH // 4, (first + eighths) * EIGHTH // 4)
+                engine_copy(out=grouped_of[c][:].rearrange("p (r i) t -> p r t i", i=4)[:, runs],
+                            in_=raw[:, :, col:col + CHUNK].rearrange("p t (r i) -> p r t i", i=4)[:, runs])
+            eighths_done[c] += eighths
+            while len(issued) < len(loads) and all(eighths_done.get(x, 0) == EIGHTHS
                                                    for x in chunks_of_load[len(issued) - RAW_SLOTS]):
                 load_next()
 
@@ -190,24 +215,33 @@ def tile_linearattention_pb_t_kernel(tc, h_attn, xn, Wout, bout, outnorm_g, out)
                 for j in range(BLOCKS):
                     nc.vector.bn_stats(out=stats_of[c // 2][:, (c % 2) * BLOCKS + j, :], in_=fwd_of[c][:, j, :])
 
-        def small_first(pair):
-            if 0 <= pair < N_PAIRS:
+        diff_of, diff2_of, cvar_of = {}, {}, {}
+
+        def is_pair(pair):
+            return 0 <= pair < N_PAIRS
+
+        def small_a(pair):
+            if is_pair(pair):
                 st = stats_of[pair]
-                both = small.tile([P, PAIR_BLOCKS, 3], F32, name="both", tag="both")
-                nc.vector.tensor_reduce(out=both[:], in_=st[:].rearrange("p b (h s) -> p b s h", h=2),
+                diff_of[pair] = small.tile([P, PAIR_BLOCKS], F32, name="d", tag="d")
+                nc.vector.tensor_tensor(out=diff_of[pair][:], in0=st[:, :, 1], in1=st[:, :, 4], op=ALU.subtract)
+                mean2_of[pair] = small.tile([P, PAIR_BLOCKS, 3], F32, name="both", tag="both")
+                nc.vector.tensor_reduce(out=mean2_of[pair][:], in_=st[:].rearrange("p b (h s) -> p b s h", h=2),
                                         axis=AX.X, op=ALU.add)
-                d = small.tile([P, PAIR_BLOCKS], F32, name="d", tag="d")
-                nc.vector.tensor_tensor(out=d[:], in0=st[:, :, 1], in1=st[:, :, 4], op=ALU.subtract)
-                dd = small.tile([P, PAIR_BLOCKS], F32, name="dd", tag="dd")
-                nc.vector.tensor_tensor(out=dd[:], in0=d[:], in1=d[:], op=ALU.mult)
-                c_var = small.tile([P, PAIR_BLOCKS], F32, name="c_var", tag="c_var")
-                nc.vector.scalar_tensor_tensor(out=c_var[:], in0=dd[:], scalar=C / 4.0, in1=both[:, :, 2],
-                                               op0=ALU.mult, op1=ALU.add)
-                rstd = small.tile([P, PAIR_BLOCKS], F32, name="rstd", tag="rstd")
-                nc.scalar.activation(out=rstd[:], in_=c_var[:], func=ACT.Abs_reciprocal_sqrt,
+
+        def small_b(pair):
+            if is_pair(pair):
+                diff2_of[pair] = small.tile([P, PAIR_BLOCKS], F32, name="dd", tag="dd")
+                nc.vector.tensor_tensor(out=diff2_of[pair][:], in0=diff_of[pair][:], in1=diff_of[pair][:], op=ALU.mult)
+
+        def small_c(pair):
+            if is_pair(pair):
+                cvar_of[pair] = small.tile([P, PAIR_BLOCKS], F32, name="c_var", tag="c_var")
+                nc.vector.scalar_tensor_tensor(out=cvar_of[pair][:], in0=diff2_of[pair][:], scalar=C / 4.0,
+                                               in1=mean2_of[pair][:, :, 2], op0=ALU.mult, op1=ALU.add)
+                rstd_of[pair] = small.tile([P, PAIR_BLOCKS], F32, name="rstd", tag="rstd")
+                nc.scalar.activation(out=rstd_of[pair][:], in_=cvar_of[pair][:], func=ACT.Abs_reciprocal_sqrt,
                                      bias=eps_col[:], scale=1.0 / C)
-                mean2_of[pair] = both
-                rstd_of[pair] = rstd
 
         def small_second(pair):
             if 0 <= pair < N_PAIRS:
@@ -244,24 +278,31 @@ def tile_linearattention_pb_t_kernel(tc, h_attn, xn, Wout, bout, outnorm_g, out)
                     nc.sync.dma_start(out=out[b].rearrange("c h w -> c (h w)")[:, n0:n0 + width],
                                       in_=result_of[s][:])
 
-        for r in range(-AHEAD_REGROUP, N_PAIRS + 1):
-            to_regroup = [c for c in (2 * (r + AHEAD_REGROUP), 2 * (r + AHEAD_REGROUP) + 1) if exists(c)]
-            scalar_quarters = [(c, q) for c in to_regroup if not regroups_on_vector(c) for q in range(4)]
+        def one_round(r):
+            work = [(c,) + piece for c in (2 * (r + AHEAD_REGROUP), 2 * (r + AHEAD_REGROUP) + 1) if exists(c)
+                    for piece in shares(c)]
             even, odd = 2 * r, 2 * r + 1
 
-            small_first(r)
-            for c in to_regroup:
-                if regroups_on_vector(c):
-                    regroup(c, nc.vector.tensor_copy, 0, 4)
+            own = [piece for piece in work if piece[1] == "vector"]
+            small_a(r)
+            for c, engine, first, eighths in own[:1]:
+                regroup(c, engine, first, eighths)
+            small_b(r)
+            for c, engine, first, eighths in own[1:]:
+                regroup(c, engine, first, eighths)
+            small_c(r)
             quantise(even + 2 * AHEAD_QUANTISE)
-            for c, q in scalar_quarters[:1]:
-                regroup(c, nc.scalar.copy, q, 1)
             small_second(r)
             quantise(odd + 2 * AHEAD_QUANTISE)
+            for c, engine, first, eighths in work:
+                if engine == "gpsimd":
+                    regroup(c, engine, first, eighths)
             multiply(even + 2 * AHEAD_MULTIPLY)
             multiply(odd + 2 * AHEAD_MULTIPLY)
             normalise(even)
             normalise(odd)
+            stats(even + 2 * AHEAD_STATS)
+            stats(odd + 2 * AHEAD_STATS)
             last(even - 2)
             last(odd - 2)
             backward(even)
@@ -270,9 +311,16 @@ def tile_linearattention_pb_t_kernel(tc, h_attn, xn, Wout, bout, outnorm_g, out)
             forward(even + 2 * AHEAD_MULTIPLY)
             add_bias(odd + 2 * AHEAD_MULTIPLY)
             forward(odd + 2 * AHEAD_MULTIPLY)
-            stats(even + 2 * AHEAD_STATS)
-            stats(odd + 2 * AHEAD_STATS)
             if (r + 5) % 4 == 0:
                 load_residual((r + 5) // 4)
-            for c, q in scalar_quarters[1:]:
-                regroup(c, nc.scalar.copy, q, 1)
+            for c, engine, first, eighths in work:
+                if engine == "scalar":
+                    regroup(c, engine, first, eighths)
+
+        for r in range(-AHEAD_REGROUP, FIRST_PINNED):
+            one_round(r)
+        with tc.manual_schedule(engines={mybir.EngineType.DVE}):
+            for r in range(FIRST_PINNED, LAST_PINNED + 1):
+                one_round(r)
+        for r in range(LAST_PINNED + 1, N_PAIRS + 1):
+            one_round(r)

@@ -32,8 +32,7 @@ AHEAD_STATS = 1
 BIG_LOAD = 2048
 RAW_SLOTS = 4
 VECTOR_EIGHTHS = 4
-GPSIMD_EIGHTHS = 7
-GPSIMD_PIECES = (4, 3)
+GPSIMD_PIECES = (5,)
 FIRST_PINNED = 1
 LAST_PINNED = N_PAIRS - 5
 
@@ -156,7 +155,7 @@ def tile_linearattention_pb_t_kernel(tc, h_attn, xn, Wout, bout, outnorm_g, out)
             for width in GPSIMD_PIECES:
                 pieces.append(("gpsimd", first, width))
                 first += width
-            return pieces + [("scalar", first, EIGHTHS - first)]
+            return pieces + [("scalar", first, 1)] + [("scalar", e, 2) for e in range(first + 1, EIGHTHS, 2)]
 
         def regroup(c, engine, first, eighths):
             if c not in grouped_of:

@@ -31,8 +31,8 @@ AHEAD_MULTIPLY = 2
 AHEAD_STATS = 1
 BIG_LOAD = 2048
 RAW_SLOTS = 4
-VECTOR_EIGHTHS = 4
-GPSIMD_PIECES = (5,)
+VECTOR_EIGHTHS = 6
+GPSIMD_PIECES = (3,)
 FIRST_PINNED = 1
 LAST_PINNED = N_PAIRS - 5
 

@@ -17,8 +17,8 @@ IMAGES, C, K, N = 4, 128, 512, 4096
 PACK = 4
 CHUNK = 512
 BLOCKS = CHUNK // P
-EIGHTH = CHUNK // 8
-EIGHTHS = 8
+EIGHTH = CHUNK // 16
+EIGHTHS = 16
 N_CHUNKS = IMAGES * N // CHUNK
 N_PAIRS = N_CHUNKS // 2
 PAIR_BLOCKS = 2 * BLOCKS
@@ -31,8 +31,9 @@ AHEAD_MULTIPLY = 2
 AHEAD_STATS = 1
 BIG_LOAD = 2048
 RAW_SLOTS = 4
-VECTOR_EIGHTHS = 6
-GPSIMD_PIECES = (3,)
+VECTOR_PIECES = (4, 4, 3)
+GPSIMD_PIECES = (8,)
+SCALAR_PIECE = 4
 FIRST_PINNED = 1
 LAST_PINNED = N_PAIRS - 5
 
@@ -148,14 +149,15 @@ def tile_linearattention_pb_t_kernel(tc, h_attn, xn, Wout, bout, outnorm_g, out)
         def shares(c):
             if c < 2:
                 return [("vector", 0, EIGHTHS)]
-            if c % 2 == 0:
-                return ([("vector", e, 2) for e in range(0, VECTOR_EIGHTHS, 2)]
-                        + [("scalar", e, 2) for e in range(VECTOR_EIGHTHS, EIGHTHS, 2)])
             pieces, first = [], 0
-            for width in GPSIMD_PIECES:
-                pieces.append(("gpsimd", first, width))
+            for width in (VECTOR_PIECES if c % 2 == 0 else GPSIMD_PIECES):
+                pieces.append(("vector" if c % 2 == 0 else "gpsimd", first, width))
                 first += width
-            return pieces + [("scalar", first, 1)] + [("scalar", e, 2) for e in range(first + 1, EIGHTHS, 2)]
+            while first < EIGHTHS:
+                width = min(SCALAR_PIECE, EIGHTHS - first)
+                pieces.append(("scalar", first, width))
+                first += width
+            return pieces
 
         def regroup(c, engine, first, eighths):
             if c not in grouped_of:

@@ -57,7 +57,7 @@ def tile_linearattention_pb_t_kernel(tc, h_attn, xn, Wout, bout, outnorm_g, out)
         psum_back = ctx.enter_context(tc.psum_pool(name="psum_back", bufs=2))
 
         w_sb = const.tile([P, K], BF16)
-        nc.scalar.dma_start(out=w_sb[:], in_=Wout)
+        nc.sync.dma_start(out=w_sb[:], in_=Wout)
         vec_rows = const.tile([P, P], BF16)
         nc.vector.memset(vec_rows[:], 0.0)
         nc.scalar.dma_start(out=vec_rows[0:1, :], in_=bout.unsqueeze(0))
@@ -147,11 +147,10 @@ def tile_linearattention_pb_t_kernel(tc, h_attn, xn, Wout, bout, outnorm_g, out)
             return 0 <= c < N_CHUNKS
 
         def shares(c):
-            if c < 2:
-                return [("vector", 0, EIGHTHS)]
+            by_vector = c % 2 == 0 or c < 2
             pieces, first = [], 0
-            for width in (VECTOR_PIECES if c % 2 == 0 else GPSIMD_PIECES):
-                pieces.append(("vector" if c % 2 == 0 else "gpsimd", first, width))
+            for width in (VECTOR_PIECES if by_vector else GPSIMD_PIECES):
+                pieces.append(("vector" if by_vector else "gpsimd", first, width))
                 first += width
             while first < EIGHTHS:
                 width = min(SCALAR_PIECE, EIGHTHS - first)

@@ -31,8 +31,8 @@ AHEAD_MULTIPLY = 2
 AHEAD_STATS = 1
 BIG_LOAD = 2048
 RAW_SLOTS = 4
-VECTOR_PIECES = (4, 4, 3)
-GPSIMD_PIECES = (8,)
+VECTOR_PIECES = (5, 4)
+GPSIMD_PIECES = (11,)
 SCALAR_PIECE = 4
 FIRST_PINNED = 1
 LAST_PINNED = N_PAIRS - 5

from contextlib import ExitStack

import concourse.mybir as mybir
from concourse.masks import make_identity

F32 = mybir.dt.float32
BF16 = mybir.dt.bfloat16
U32 = mybir.dt.uint32
U8 = mybir.dt.uint8
FP8X4 = mybir.dt.float8_e4m3fn_x4
ALU = mybir.AluOpType
ACT = mybir.ActivationFunctionType
AX = mybir.AxisListType

P = 128
IMAGES, C, K, N = 4, 128, 512, 4096
PACK = 4
CHUNK = 512
BLOCKS = CHUNK // P
EIGHTH = CHUNK // 16
EIGHTHS = 16
N_CHUNKS = IMAGES * N // CHUNK
N_PAIRS = N_CHUNKS // 2
PAIR_BLOCKS = 2 * BLOCKS
EPS = 1e-5
FLOPS = 2 * C * K * IMAGES * N

AHEAD_REGROUP = 4
AHEAD_QUANTISE = 3
AHEAD_MULTIPLY = 2
AHEAD_STATS = 1
BIG_LOAD = 2048
RAW_SLOTS = 4
VECTOR_PIECES = (5, 4)
GPSIMD_PIECES = (11,)
SCALAR_PIECE = 4
FIRST_PINNED = 1
LAST_PINNED = N_PAIRS - 5


def tile_linearattention_pb_t_kernel(tc, h_attn, xn, Wout, bout, outnorm_g, out):
    nc = tc.nc
    with ExitStack() as ctx:
        const = ctx.enter_context(tc.tile_pool(name="const", bufs=1))
        raw_small = ctx.enter_context(tc.tile_pool(name="raw_small", bufs=4))
        raw_big = ctx.enter_context(tc.tile_pool(name="raw_big", bufs=RAW_SLOTS))
        resid = ctx.enter_context(tc.tile_pool(name="resid", bufs=3))
        grouped_even = ctx.enter_context(tc.tile_pool(name="grouped_even", bufs=2))
        grouped_odd = ctx.enter_context(tc.tile_pool(name="grouped_odd", bufs=1))
        quantised = ctx.enter_context(tc.tile_pool(name="quantised", bufs=2 * AHEAD_QUANTISE))
        biased = ctx.enter_context(tc.tile_pool(name="biased", bufs=4))
        normed = ctx.enter_context(tc.tile_pool(name="normed", bufs=4))
        result = ctx.enter_context(tc.tile_pool(name="result", bufs=3))
        small = ctx.enter_context(tc.tile_pool(name="small", bufs=3))
        psum_y = ctx.enter_context(tc.psum_pool(name="psum_y", bufs=2))
        psum_fwd = ctx.enter_context(tc.psum_pool(name="psum_fwd", bufs=4))
        psum_back = ctx.enter_context(tc.psum_pool(name="psum_back", bufs=2))

        w_sb = const.tile([P, K], BF16)
        nc.sync.dma_start(out=w_sb[:], in_=Wout)
        vec_rows = const.tile([P, P], BF16)
        nc.vector.memset(vec_rows[:], 0.0)
        nc.scalar.dma_start(out=vec_rows[0:1, :], in_=bout.unsqueeze(0))
        nc.scalar.dma_start(out=vec_rows[1:2, :], in_=outnorm_g.rearrange("a c h w -> (a h w) c"))

        loads = []
        for b in range(IMAGES):
            widths = (CHUNK,) * 4 + (BIG_LOAD,) if b == 0 else (BIG_LOAD,) * 2
            n0 = 0
            for width in widths:
                loads.append((b, n0, width))
                n0 += width
        chunks_of_load = [[(b * N + n0) // CHUNK + j for j in range(width // CHUNK)] for (b, n0, width) in loads]
        raw_of = {}
        eighths_done = {}
        resid_of = {}
        issued = []

        def load_next():
            b, n0, width = loads[len(issued)]
            if width == CHUNK:
                raw = raw_small.tile([P, PACK, width], BF16, name="raw_s", tag="raw_s")
            else:
                raw = raw_big.tile([P, PACK, width], BF16, name="raw_b", tag="raw_b")
            rows = h_attn[b].rearrange("(p t) h w -> p t (h w)", t=PACK)
            nc.sync.dma_start(out=raw[:], in_=rows[:, :, n0:n0 + width])
            for j, c in enumerate(chunks_of_load[len(issued)]):
                raw_of[c] = (raw, j * CHUNK)
            issued.append(raw)

        def load_residual(b):
            if b < IMAGES:
                xt = resid.tile([P, N], BF16, name="xt", tag="xt")
                nc.sync.dma_start(out=xt[:], in_=xn[b].rearrange("c h w -> c (h w)"))
                resid_of[b] = xt

        eps_col = const.tile([P, 1], F32)
        nc.vector.memset(eps_col[:], EPS)
        warm = const.tile([P, 1], F32)
        nc.scalar.activation(out=warm[:], in_=eps_col[:], func=ACT.Abs_reciprocal_sqrt)
        ident_b = const.tile([P, P], BF16)
        make_identity(nc, ident_b[:])
        ident_f = const.tile([P, P], F32)
        make_identity(nc, ident_f[:])

        while len(issued) < len(loads) and loads[len(issued)][0] == 0:
            load_next()
        load_residual(0)
        for i in range(RAW_SLOTS - 1):
            load_next()

        w_split = const.tile([P, PACK, P], BF16)
        nc.vector.tensor_copy(out=w_split[:], in_=w_sb[:].rearrange("c (p t) -> c t p", t=PACK))
        w_ps = psum_back.tile([P, PACK, P], BF16, name="w_ps", tag="back")
        for t in range(PACK):
            nc.tensor.transpose(w_ps[:, t, :], w_split[:, t, :], ident_b[:])
        w_grouped = const.tile([P, C, PACK], BF16, align_bytes=64)
        nc.vector.tensor_copy(out=w_grouped[:], in_=w_ps[:].rearrange("p t c -> p c t"))
        w_words = const.tile([P, C], U32, align_bytes=64)
        w_scales = const.tile([P, C], U8, align_bytes=64)
        nc.vector.quantize_mx(out=w_words[:].bitcast(FP8X4), scales=w_scales[:],
                              in_=w_grouped[:].rearrange("p c t -> p (c t)"))
        vec_ps = psum_back.tile([P, P], BF16, name="vec_ps", tag="back")
        nc.tensor.transpose(vec_ps[:], vec_rows[:], ident_b[:])
        vec_cols = const.tile([P, 2], F32)
        nc.vector.tensor_copy(out=vec_cols[:], in_=vec_ps[:, 0:2])
        bias_col = vec_cols[:, 0:1]
        gain_col = vec_cols[:, 1:2]

        stores = []
        for b in range(IMAGES):
            widths = (BIG_LOAD, 2 * CHUNK, CHUNK, CHUNK) if b == IMAGES - 1 else (BIG_LOAD,) * 2
            n0 = 0
            for width in widths:
                stores.append((b, n0, width))
                n0 += width
        store_of = {}
        for s, (b, n0, width) in enumerate(stores):
            for j in range(width // CHUNK):
                store_of[(b * N + n0) // CHUNK + j] = (s, j * CHUNK, j == width // CHUNK - 1)
        result_of = {}

        grouped_of, words_of, y_of, biased_of, fwd_of, normed_of, back_of = {}, {}, {}, {}, {}, {}, {}
        stats_of, mean2_of, rstd_of, shift_of = {}, {}, {}, {}

        def exists(c):
            return 0 <= c < N_CHUNKS

        def shares(c):
            by_vector = c % 2 == 0 or c < 2
            pieces, first = [], 0
            for width in (VECTOR_PIECES if by_vector else GPSIMD_PIECES):
                pieces.append(("vector" if by_vector else "gpsimd", first, width))
                first += width
            while first < EIGHTHS:
                width = min(SCALAR_PIECE, EIGHTHS - first)
                pieces.append(("scalar", first, width))
                first += width
            return pieces

        def regroup(c, engine, first, eighths):
            if c not in grouped_of:
                if c % 2 == 0:
                    grouped_of[c] = grouped_even.tile([P, CHUNK, PACK], BF16, name="g0", tag="g0", align_bytes=64)
                else:
                    grouped_of[c] = grouped_odd.tile([P, CHUNK, PACK], BF16, name="g1", tag="g1", align_bytes=64)
                eighths_done[c] = 0
            raw, col = raw_of[c]
            if engine == "gpsimd":
                n0, n1 = first * EIGHTH, (first + eighths) * EIGHTH
                nc.gpsimd.tensor_scalar(out=grouped_of[c][:, n0:n1, :],
                                        in0=raw[:, :, col + n0:col + n1].rearrange("p t n -> p n t"),
                                        scalar1=1.0, scalar2=0.0, op0=ALU.mult, op1=ALU.add)
            else:
                engine_copy = nc.vector.tensor_copy if engine == "vector" else nc.scalar.copy
                runs = slice(first * EIGHTH // 4, (first + eighths) * EIGHTH // 4)
                engine_copy(out=grouped_of[c][:].rearrange("p (r i) t -> p r t i", i=4)[:, runs],
                            in_=raw[:, :, col:col + CHUNK].rearrange("p t (r i) -> p r t i", i=4)[:, runs])
            eighths_done[c] += eighths
            while len(issued) < len(loads) and all(eighths_done.get(x, 0) == EIGHTHS
                                                   for x in chunks_of_load[len(issued) - RAW_SLOTS]):
                load_next()

        def quantise(c):
            if exists(c):
                words = quantised.tile([P, CHUNK], U32, name="words", tag="words", align_bytes=64)
                scales = quantised.tile([P, CHUNK], U8, name="scales", tag="scales", align_bytes=64)
                nc.vector.quantize_mx(out=words[:].bitcast(FP8X4), scales=scales[:],
                                      in_=grouped_of[c][:].rearrange("p n t -> p (n t)"))
                words_of[c] = (words, scales)

        def multiply(c):
            if exists(c):
                words, scales = words_of[c]
                y_of[c] = psum_y.tile([P, CHUNK], F32, name="y", tag="y")
                nc.tensor.matmul_mx(out=y_of[c][:], lhsT=w_words[:].bitcast(FP8X4), lhsT_scale=w_scales[:],
                                    rhs=words[:].bitcast(FP8X4), rhs_scale=scales[:], start=True, stop=True)

        def add_bias(c):
            if exists(c):
                biased_of[c] = biased.tile([P, CHUNK], F32, name="t", tag="t")
                nc.scalar.activation(out=biased_of[c][:], in_=y_of[c][:], func=ACT.Identity,
                                     bias=bias_col, scale=1.0)

        def forward(c):
            if exists(c):
                fwd_of[c] = psum_fwd.tile([P, BLOCKS, P], F32, name="fwd", tag="fwd")
                for j in range(BLOCKS):
                    nc.tensor.transpose(fwd_of[c][:, j, :], biased_of[c][:, j * P:(j + 1) * P], ident_f[:])

        def stats(c):
            if exists(c):
                if c // 2 not in stats_of:
                    stats_of[c // 2] = small.tile([P, PAIR_BLOCKS, 6], F32, name="st", tag="st")
                for j in range(BLOCKS):
                    nc.vector.bn_stats(out=stats_of[c // 2][:, (c % 2) * BLOCKS + j, :], in_=fwd_of[c][:, j, :])

        diff_of, diff2_of, cvar_of = {}, {}, {}

        def is_pair(pair):
            return 0 <= pair < N_PAIRS

        def small_a(pair):
            if is_pair(pair):
                st = stats_of[pair]
                diff_of[pair] = small.tile([P, PAIR_BLOCKS], F32, name="d", tag="d")
                nc.vector.tensor_tensor(out=diff_of[pair][:], in0=st[:, :, 1], in1=st[:, :, 4], op=ALU.subtract)
                mean2_of[pair] = small.tile([P, PAIR_BLOCKS, 3], F32, name="both", tag="both")
                nc.vector.tensor_reduce(out=mean2_of[pair][:], in_=st[:].rearrange("p b (h s) -> p b s h", h=2),
                                        axis=AX.X, op=ALU.add)

        def small_b(pair):
            if is_pair(pair):
                diff2_of[pair] = small.tile([P, PAIR_BLOCKS], F32, name="dd", tag="dd")
                nc.vector.tensor_tensor(out=diff2_of[pair][:], in0=diff_of[pair][:], in1=diff_of[pair][:], op=ALU.mult)

        def small_c(pair):
            if is_pair(pair):
                cvar_of[pair] = small.tile([P, PAIR_BLOCKS], F32, name="c_var", tag="c_var")
                nc.vector.scalar_tensor_tensor(out=cvar_of[pair][:], in0=diff2_of[pair][:], scalar=C / 4.0,
                                               in1=mean2_of[pair][:, :, 2], op0=ALU.mult, op1=ALU.add)
                rstd_of[pair] = small.tile([P, PAIR_BLOCKS], F32, name="rstd", tag="rstd")
                nc.scalar.activation(out=rstd_of[pair][:], in_=cvar_of[pair][:], func=ACT.Abs_reciprocal_sqrt,
                                     bias=eps_col[:], scale=1.0 / C)

        def small_second(pair):
            if 0 <= pair < N_PAIRS:
                shift_of[pair] = small.tile([P, PAIR_BLOCKS], F32, name="shift", tag="shift")
                nc.vector.scalar_tensor_tensor(out=shift_of[pair][:], in0=mean2_of[pair][:, :, 1], scalar=-0.5,
                                               in1=rstd_of[pair][:], op0=ALU.mult, op1=ALU.mult)

        def normalise(c):
            if exists(c):
                rstd, shift = rstd_of[c // 2], shift_of[c // 2]
                normed_of[c] = normed.tile([P, BLOCKS, P], F32, name="z", tag="z")
                for j in range(BLOCKS):
                    col = (c % 2) * BLOCKS + j
                    nc.scalar.activation(out=normed_of[c][:, j, :], in_=fwd_of[c][:, j, :], func=ACT.Identity,
                                         bias=shift[:, col:col + 1], scale=rstd[:, col:col + 1])

        def backward(c):
            if exists(c):
                back_of[c] = psum_back.tile([P, CHUNK], F32, name="back", tag="back")
                for j in range(BLOCKS):
                    nc.tensor.transpose(back_of[c][:, j * P:(j + 1) * P], normed_of[c][:, j, :], ident_f[:])

        def last(c):
            if exists(c):
                s, col, completes = store_of[c]
                b, n0, width = stores[s]
                if s not in result_of:
                    result_of[s] = result.tile([P, width], F32, name="o", tag="o")
                n = c * CHUNK - b * N
                nc.vector.scalar_tensor_tensor(out=result_of[s][:, col:col + CHUNK], in0=back_of[c][:],
                                               scalar=gain_col, in1=resid_of[b][:, n:n + CHUNK],
                                               op0=ALU.mult, op1=ALU.add)
                if completes:
                    nc.sync.dma_start(out=out[b].rearrange("c h w -> c (h w)")[:, n0:n0 + width],
                                      in_=result_of[s][:])

        def one_round(r):
            work = [(c,) + piece for c in (2 * (r + AHEAD_REGROUP), 2 * (r + AHEAD_REGROUP) + 1) if exists(c)
                    for piece in shares(c)]
            even, odd = 2 * r, 2 * r + 1

            own = [piece for piece in work if piece[1] == "vector"]
            small_a(r)
            for c, engine, first, eighths in own[:1]:
                regroup(c, engine, first, eighths)
            small_b(r)
            for c, engine, first, eighths in own[1:]:
                regroup(c, engine, first, eighths)
            small_c(r)
            quantise(even + 2 * AHEAD_QUANTISE)
            small_second(r)
            quantise(odd + 2 * AHEAD_QUANTISE)
            for c, engine, first, eighths in work:
                if engine == "gpsimd":
                    regroup(c, engine, first, eighths)
            multiply(even + 2 * AHEAD_MULTIPLY)
            multiply(odd + 2 * AHEAD_MULTIPLY)
            normalise(even)
            normalise(odd)
            stats(even + 2 * AHEAD_STATS)
            stats(odd + 2 * AHEAD_STATS)
            last(even - 2)
            last(odd - 2)
            backward(even)
            backward(odd)
            add_bias(even + 2 * AHEAD_MULTIPLY)
            forward(even + 2 * AHEAD_MULTIPLY)
            add_bias(odd + 2 * AHEAD_MULTIPLY)
            forward(odd + 2 * AHEAD_MULTIPLY)
            if (r + 5) % 4 == 0:
                load_residual((r + 5) // 4)
            for c, engine, first, eighths in work:
                if engine == "scalar":
                    regroup(c, engine, first, eighths)

        for r in range(-AHEAD_REGROUP, FIRST_PINNED):
            one_round(r)
        with tc.manual_schedule(engines={mybir.EngineType.DVE}):
            for r in range(FIRST_PINNED, LAST_PINNED + 1):
                one_round(r)
        for r in range(LAST_PINNED + 1, N_PAIRS + 1):
            one_round(r)
